import numpy as np
import ml_dtypes


def mxq(x, axis, fmt="e4m3"):
    dtype, down = {"e4m3": (ml_dtypes.float8_e4m3fn, 7), "e5m2": (ml_dtypes.float8_e5m2, 14)}[fmt]
    v = np.moveaxis(np.asarray(x, np.float32).astype(ml_dtypes.bfloat16).astype(np.float64), axis, -1)
    blocks = v.reshape(v.shape[:-1] + (-1, 32))
    amax = np.abs(blocks).max(-1, keepdims=True)
    byte = np.maximum(np.where(amax > 0, np.frexp(amax)[1] - 1 + 127, 0) - down, 1)
    scale = np.exp2(byte - 127.0)
    codes = (blocks / scale).astype(np.float32).astype(dtype).astype(np.float64)
    return np.moveaxis((codes * scale).reshape(v.shape), -1, axis)


WIDE = False


def mx_kscale(k):
    if not WIDE:
        return np.ones(k)
    levels = np.array([10, -10, 5, -5, 0])
    a = np.random.permutation(np.resize(levels, k // 512 * 4)).reshape(k // 512, 4)
    idx = np.arange(k)
    return np.exp2(a[idx // 512, idx % 128 // 32])


BF16 = ml_dtypes.bfloat16


def bf(x):
    return np.asarray(x, np.float32).astype(BF16)


def f64(x):
    return np.asarray(x).astype(np.float64)


B, S, V, C, D = 4, 512, 4096, 128, 512
EPS_SINK = 0.05
TEMP = 1.0


def l2norm(t):
    n = np.sqrt(np.sum(t * t, axis=1, keepdims=True))
    return t / np.maximum(n, 1e-12)


def sigmoid(v):
    return 1.0 / (1.0 + np.exp(-v))


def setup_inputs():
    s = mx_kscale(S)
    return {"x": bf(np.random.standard_normal((B, S, V)) * s[None, :, None]),
            "cluster_emb": bf(np.random.standard_normal((C, D)) * 3.0),
            "W": bf(np.random.standard_normal((D, S)) * 2.0 / np.sqrt(S) / s[None, :]),
            "b": bf(np.random.standard_normal(D) * 0.5),
            "noise": bf(np.clip(np.random.uniform(size=(V, C)), 0.004, 0.996))}


def reference(x, cluster_emb, W, b, noise):
    x_emb = (mxq(f64(x), 1, "e4m3").transpose(0, 2, 1) @ mxq(f64(W), 1, "e4m3").T) + f64(b)
    xf = x_emb.reshape(-1, D)
    cn = l2norm(f64(cluster_emb))
    prob = (mxq(l2norm(xf), 1, "e4m3") @ mxq(cn, 1, "e4m3").T).reshape(B, V, C)
    prob_avg = np.mean(prob, axis=0)
    Q = np.exp(prob_avg / EPS_SINK)
    prob_avg = Q / np.sum(Q, axis=1, keepdims=True)
    u = f64(noise)
    logit_noise = np.log(u) - np.log(1.0 - u)
    logit_p = np.log(prob_avg + 1e-10) - np.log(1.0 - prob_avg + 1e-10)
    mask = sigmoid((logit_p + logit_noise) / TEMP)
    return prob_avg, mask

@@ -1,0 +1,254 @@
+from contextlib import ExitStack
+
+import concourse.mybir as mybir
+from concourse.masks import make_identity
+
+F32 = mybir.dt.float32
+BF16 = mybir.dt.bfloat16
+U32 = mybir.dt.uint32
+U8 = mybir.dt.uint8
+FP8X4 = mybir.dt.float8_e4m3fn_x4
+ALU = mybir.AluOpType
+ACT = mybir.ActivationFunctionType
+
+P = 128
+NB = 4
+S = 512
+V = 4096
+C = 128
+D = 512
+VB = 512
+NVB = V // VB
+TPB = VB // P
+UNITS = V // P
+EPS = 1e-10
+
+FLOPS = 2 * NB * V * S * D + 2 * NB * V * D * C
+
+
+def tile_cluster_assigner_pa_t_kernel(tc, x, cluster_emb, W, b, noise, out_0, out_1):
+    nc = tc.nc
+    with ExitStack() as ctx:
+        const = ctx.enter_context(tc.tile_pool(name="const", bufs=1))
+        rawp = ctx.enter_context(tc.tile_pool(name="rawp", bufs=8))
+        xgp = ctx.enter_context(tc.tile_pool(name="xgp", bufs=2))
+        xcp = ctx.enter_context(tc.tile_pool(name="xcp", bufs=8))
+        xep = ctx.enter_context(tc.tile_pool(name="xep", bufs=3))
+        work = ctx.enter_context(tc.tile_pool(name="work", bufs=2))
+        small = ctx.enter_context(tc.tile_pool(name="small", bufs=4))
+        epi = ctx.enter_context(tc.tile_pool(name="epi", bufs=2))
+        pse = ctx.enter_context(tc.psum_pool(name="pse", bufs=4))
+        pst = ctx.enter_context(tc.psum_pool(name="pst", bufs=2))
+        psm = ctx.enter_context(tc.psum_pool(name="psm", bufs=2))
+
+        raws = {}
+        xcodes = {}
+
+        def load_x(k):
+            vb, n = divmod(k, NB)
+            raw = rawp.tile([P, 4, VB], BF16, name="raw")
+            nc.sync.dma_start(
+                out=raw[:],
+                in_=x[n, :, vb * VB : (vb + 1) * VB].rearrange("(p j) w -> p j w", j=4),
+            )
+            raws[k] = raw
+
+        def prep_x(k):
+            raw = raws.pop(k)
+            g = xgp.tile([P, VB, 4], BF16, name="xg", align_bytes=64)
+            nc.vector.tensor_copy(
+                out=g[:].rearrange("p (c i) t -> p c t i", i=4),
+                in_=raw[:].rearrange("p t (c i) -> p c t i", i=4),
+            )
+            codes = xcp.tile([P, VB], U32, name="xcodes", align_bytes=64)
+            scales = xcp.tile([P, VB], U8, name="xscales", align_bytes=64)
+            nc.vector.quantize_mx(
+                out=codes[:].bitcast(FP8X4),
+                scales=scales[:],
+                in_=g[:].rearrange("p w t -> p (w t)"),
+            )
+            xcodes[k] = (codes, scales)
+
+        w_sb = const.tile([P, 4, S], BF16, name="w_sb")
+        nc.sync.dma_start(out=w_sb[:], in_=W.rearrange("(a p) t -> p a t", p=P))
+        for k in range(8):
+            load_x(k)
+        ce = const.tile([P, D], BF16, name="ce")
+        nc.scalar.dma_start(out=ce[:], in_=cluster_emb)
+        b_bc = const.tile([P, D], BF16, name="b_bc")
+        nc.scalar.dma_start(out=b_bc[:], in_=b.partition_broadcast(P))
+        u = const.tile([P, UNITS, C], BF16, name="u")
+        nc.gpsimd.dma_start(out=u[:], in_=noise.rearrange("(t p) c -> p t c", p=P))
+
+        ident = const.tile([P, P], BF16, name="ident")
+        make_identity(nc, ident[:])
+        mhalf = const.tile([P, 4], F32, name="mhalf")
+        nc.vector.memset(mhalf[:], -0.5)
+
+        gw = const.tile([P, 4, P, 4], BF16, name="gw", align_bytes=64)
+        for h in range(2):
+            wt = pst.tile([P, 2, 4, P], BF16, name="xt")
+            for a2 in range(2):
+                for j in range(4):
+                    nc.tensor.transpose(
+                        wt[:, a2, j, :],
+                        w_sb[:, 2 * h + a2, :].rearrange("p (q j) -> p j q", j=4)[:, j, :],
+                        ident[:],
+                    )
+            nc.vector.tensor_copy(
+                out=gw[:, 2 * h : 2 * h + 2, :, :], in_=wt[:].rearrange("p a j d -> p a d j")
+            )
+        wc = const.tile([P, D], U32, name="wc", align_bytes=64)
+        ws = const.tile([P, D], U8, name="ws", align_bytes=64)
+        nc.vector.quantize_mx(
+            out=wc[:].bitcast(FP8X4), scales=ws[:], in_=gw[:].rearrange("p a d j -> p (a d j)")
+        )
+
+        def rsqrt_clamped(out, in_, width):
+            cl = small.tile([P, 4], F32, name="cl")
+            nc.gpsimd.tensor_scalar(
+                out=cl[:, 0:width], in0=in_, scalar1=3.0e38, scalar2=1e-24, op0=ALU.min, op1=ALU.max
+            )
+            nc.gpsimd.tensor_tensor(out=out, in0=cl[:, 0:width], in1=mhalf[:, 0:width], op=ALU.pow)
+
+        junk0 = work.tile([P, D], BF16, name="junk")
+        ssc = small.tile([P, 4], F32, name="ss")
+        nc.scalar.activation(out=junk0[:], in_=ce[:], func=ACT.Square, accum_out=ssc[:, 0:1])
+        rc = small.tile([P, 4], F32, name="rn")
+        rsqrt_clamped(rc[:, 0:1], ssc[:, 0:1], 1)
+        cn = const.tile([P, D], BF16, name="cn")
+        nc.vector.tensor_scalar(out=cn[:], in0=ce[:], scalar1=rc[:, 0:1], scalar2=None, op0=ALU.mult)
+        ct = pst.tile([P, 2, 4, P], BF16, name="xt")
+        for t in range(4):
+            nc.tensor.transpose(ct[:, 0, t, :], cn[:, t * P : (t + 1) * P], ident[:])
+        gc = const.tile([P, C, 4], BF16, name="gc", align_bytes=64)
+        nc.vector.tensor_copy(out=gc[:], in_=ct[:, 0, :, :].rearrange("p t c -> p c t"))
+        cc = const.tile([P, C], U32, name="cc", align_bytes=64)
+        cs = const.tile([P, C], U8, name="cs", align_bytes=64)
+        nc.vector.quantize_mx(
+            out=cc[:].bitcast(FP8X4), scales=cs[:], in_=gc[:].rearrange("p c t -> p (c t)")
+        )
+
+        um1 = const.tile([P, UNITS, C], F32, name="um1")
+        nc.gpsimd.tensor_scalar(
+            out=um1[:], in0=u[:], scalar1=1.0, scalar2=-1.0, op0=ALU.mult, op1=ALU.add
+        )
+
+        state = {}
+
+        def stage_a(un):
+            vb, t = divmod(un, TPB)
+            xe = xep.tile([P, NB, D], F32, name="xe")
+            ss = small.tile([P, 4], F32, name="ss")
+            for n in range(NB):
+                codes, scales = xcodes[vb * NB + n]
+                e = pse.tile([P, D], F32, name="e")
+                nc.tensor.matmul_mx(
+                    out=e[:],
+                    lhsT=codes[:, t * P : (t + 1) * P].bitcast(FP8X4),
+                    lhsT_scale=scales[:, t * P : (t + 1) * P],
+                    rhs=wc[:].bitcast(FP8X4),
+                    rhs_scale=ws[:],
+                    start=True,
+                    stop=True,
+                )
+                nc.vector.tensor_tensor(out=xe[:, n, :], in0=e[:], in1=b_bc[:], op=ALU.add)
+                junk = work.tile([P, D], BF16, name="junk")
+                nc.scalar.activation(
+                    out=junk[:], in_=xe[:, n, :], func=ACT.Square, accum_out=ss[:, n : n + 1]
+                )
+            rn = small.tile([P, 4], F32, name="rn")
+            rsqrt_clamped(rn[:], ss[:], 4)
+            state[un] = (xe, rn)
+
+        def stage_b(un):
+            vb, t = divmod(un, TPB)
+            xe, rn = state.pop(un)
+            xn = work.tile([P, NB, D], BF16, name="xn")
+            for n in range(NB):
+                if n % 2 == 0:
+                    nc.vector.tensor_scalar(
+                        out=xn[:, n, :], in0=xe[:, n, :], scalar1=rn[:, n : n + 1], scalar2=None, op0=ALU.mult
+                    )
+                else:
+                    nc.scalar.activation(
+                        out=xn[:, n, :], in_=xe[:, n, :], func=ACT.Copy, scale=rn[:, n : n + 1]
+                    )
+            g2 = work.tile([P, NB, P, 4], BF16, name="g2", align_bytes=64)
+            for h in range(2):
+                xt = pst.tile([P, 2, 4, P], BF16, name="xt")
+                for n2 in range(2):
+                    for q in range(4):
+                        nc.tensor.transpose(
+                            xt[:, n2, q, :], xn[:, 2 * h + n2, q * P : (q + 1) * P], ident[:]
+                        )
+                nc.scalar.copy(
+                    out=g2[:, 2 * h : 2 * h + 2, :, :], in_=xt[:].rearrange("p n q v -> p n v q")
+                )
+            c2 = work.tile([P, NB * P], U32, name="c2", align_bytes=64)
+            s2 = work.tile([P, NB * P], U8, name="s2", align_bytes=64)
+            nc.vector.quantize_mx(
+                out=c2[:].bitcast(FP8X4), scales=s2[:], in_=g2[:].rearrange("p n v q -> p (n v q)")
+            )
+            if t == 0:
+                m4_new = psm.tile([P, TPB, C], F32, name="m4")
+                state["m4"] = m4_new
+            m4 = state["m4"]
+            for n in range(NB):
+                nc.tensor.matmul_mx(
+                    out=m4[:, t, :],
+                    lhsT=c2[:, n * P : (n + 1) * P].bitcast(FP8X4),
+                    lhsT_scale=s2[:, n * P : (n + 1) * P],
+                    rhs=cc[:].bitcast(FP8X4),
+                    rhs_scale=cs[:],
+                    start=(n == 0),
+                    stop=(n == NB - 1),
+                )
+            if vb == NVB - 1:
+                epilogue(m4, un, t, 1)
+            elif t == TPB - 1:
+                epilogue(m4, un - t, 0, TPB)
+
+        def epilogue(m4, first, t0, nt):
+            tiles = slice(first, first + nt)
+            rows = slice(first * P, (first + nt) * P)
+            q = epi.tile([P, nt, C], F32, name="q")
+            z = small.tile([P, 4], F32, name="z")
+            for t in range(nt):
+                nc.scalar.activation(
+                    out=q[:, t, :], in_=m4[:, t0 + t, :], func=ACT.Exp, scale=5.0, accum_out=z[:, t : t + 1]
+                )
+            rz = small.tile([P, 4], F32, name="rz")
+            nc.vector.reciprocal(out=rz[:, 0:nt], in_=z[:, 0:nt])
+            pa = epi.tile([P, nt, C], F32, name="pa")
+            nc.vector.tensor_tensor(
+                out=pa[:], in0=q[:], in1=rz[:, 0:nt].unsqueeze(2).to_broadcast([P, nt, C]), op=ALU.mult
+            )
+            nc.sync.dma_start(out=out_0[rows, :].rearrange("(t p) c -> p t c", p=P), in_=pa[:])
+            t1 = epi.tile([P, nt, C], F32, name="t1")
+            nc.vector.scalar_tensor_tensor(
+                out=t1[:], in0=pa[:], scalar=EPS, in1=u[:, tiles, :], op0=ALU.add, op1=ALU.mult
+            )
+            t2 = epi.tile([P, nt, C], F32, name="t2")
+            nc.vector.scalar_tensor_tensor(
+                out=t2[:], in0=pa[:], scalar=-(1.0 + EPS), in1=um1[:, tiles, :], op0=ALU.add, op1=ALU.mult
+            )
+            den = epi.tile([P, nt, C], F32, name="den")
+            nc.gpsimd.tensor_tensor(out=den[:], in0=t1[:], in1=t2[:], op=ALU.add)
+            rden = epi.tile([P, nt, C], F32, name="rden")
+            nc.vector.reciprocal(out=rden[:], in_=den[:])
+            mask = epi.tile([P, nt, C], F32, name="mask")
+            nc.gpsimd.tensor_tensor(out=mask[:], in0=t1[:], in1=rden[:], op=ALU.mult)
+            nc.sync.dma_start(out=out_1[rows, :].rearrange("(t p) c -> p t c", p=P), in_=mask[:])
+
+        for k in range(4):
+            prep_x(k)
+        for un in range(UNITS + 1):
+            if un < UNITS:
+                if un + 8 < UNITS:
+                    load_x(un + 8)
+                if un + 4 < UNITS:
+                    prep_x(un + 4)
+                stage_a(un)
+            if un >= 1:
+                stage_b(un - 1)

@@ -32,17 +32,19 @@ def tile_cluster_assigner_pa_t_kernel(tc, x, cluster_emb, W, b, noise, out_0, ou
         const = ctx.enter_context(tc.tile_pool(name="const", bufs=1))
         rawp = ctx.enter_context(tc.tile_pool(name="rawp", bufs=8))
         xgp = ctx.enter_context(tc.tile_pool(name="xgp", bufs=2))
-        xcp = ctx.enter_context(tc.tile_pool(name="xcp", bufs=8))
+        xcp = ctx.enter_context(tc.tile_pool(name="xcp", bufs=10))
         xep = ctx.enter_context(tc.tile_pool(name="xep", bufs=3))
         work = ctx.enter_context(tc.tile_pool(name="work", bufs=2))
         small = ctx.enter_context(tc.tile_pool(name="small", bufs=4))
         epi = ctx.enter_context(tc.tile_pool(name="epi", bufs=2))
         pse = ctx.enter_context(tc.psum_pool(name="pse", bufs=4))
-        pst = ctx.enter_context(tc.psum_pool(name="pst", bufs=2))
-        psm = ctx.enter_context(tc.psum_pool(name="psm", bufs=2))
+        pst = ctx.enter_context(tc.psum_pool(name="pst", bufs=3))
+        psm = ctx.enter_context(tc.psum_pool(name="psm", bufs=1))
+        ctx.enter_context(tc.manual_schedule())
 
         raws = {}
         xcodes = {}
+        st = {}
 
         def load_x(k):
             vb, n = divmod(k, NB)
@@ -69,6 +71,159 @@ def tile_cluster_assigner_pa_t_kernel(tc, x, cluster_emb, W, b, noise, out_0, ou
             )
             xcodes[k] = (codes, scales)
 
+        def rsqrt_clamped(out, in_, width):
+            cl = small.tile([P, 4], F32, name="cl")
+            nc.gpsimd.tensor_scalar(
+                out=cl[:, 0:width], in0=in_, scalar1=3.0e38, scalar2=1e-24, op0=ALU.min, op1=ALU.max
+            )
+            nc.gpsimd.tensor_tensor(out=out, in0=cl[:, 0:width], in1=mhalf[:, 0:width], op=ALU.pow)
+
+        def s1(un, n):
+            vb, t = divmod(un, TPB)
+            codes, scales = xcodes[vb * NB + n]
+            e = pse.tile([P, D], F32, name="e")
+            nc.tensor.matmul_mx(
+                out=e[:],
+                lhsT=codes[:, t * P : (t + 1) * P].bitcast(FP8X4),
+                lhsT_scale=scales[:, t * P : (t + 1) * P],
+                rhs=wc[:].bitcast(FP8X4),
+                rhs_scale=ws[:],
+                start=True,
+                stop=True,
+            )
+            st[("e", un, n)] = e
+
+        def add_square(un, n):
+            if n == 0:
+                xe_new = xep.tile([P, NB, D], F32, name="xe")
+                ss_new = small.tile([P, 4], F32, name="ss")
+                st[("xe", un)] = xe_new
+                st[("ss", un)] = ss_new
+            xe = st[("xe", un)]
+            e = st.pop(("e", un, n))
+            nc.vector.tensor_tensor(out=xe[:, n, :], in0=e[:], in1=b_bc[:], op=ALU.add)
+            junk = work.tile([P, D], BF16, name="junk")
+            nc.scalar.activation(
+                out=junk[:], in_=xe[:, n, :], func=ACT.Square, accum_out=st[("ss", un)][:, n : n + 1]
+            )
+
+        def rnorm(un):
+            rn = small.tile([P, 4], F32, name="rn")
+            rsqrt_clamped(rn[:], st.pop(("ss", un))[:], 4)
+            st[("rn", un)] = rn
+
+        def scale(un):
+            xe = st.pop(("xe", un))
+            rn = st.pop(("rn", un))
+            xn = work.tile([P, NB, D], BF16, name="xn")
+            for n in range(2):
+                nc.vector.tensor_scalar(
+                    out=xn[:, n, :], in0=xe[:, n, :], scalar1=rn[:, n : n + 1], scalar2=None, op0=ALU.mult
+                )
+            for n in range(2, NB):
+                nc.scalar.activation(
+                    out=xn[:, n, :], in_=xe[:, n, :], func=ACT.Copy, scale=rn[:, n : n + 1]
+                )
+            st[("xn", un)] = xn
+
+        def transposes(un):
+            xn = st.pop(("xn", un))
+            for h in range(2):
+                xt = pst.tile([P, 2, 4, P], BF16, name="xt")
+                for n2 in range(2):
+                    for q in range(4):
+                        nc.tensor.transpose(
+                            xt[:, n2, q, :], xn[:, 2 * h + n2, q * P : (q + 1) * P], ident[:]
+                        )
+                st[("xt", un, h)] = xt
+
+        def copy_out(un):
+            g2 = work.tile([P, NB, P, 4], BF16, name="g2", align_bytes=64)
+            for h in range(2):
+                xt = st.pop(("xt", un, h))
+                nc.scalar.copy(
+                    out=g2[:, 2 * h : 2 * h + 2, :, :], in_=xt[:].rearrange("p n q v -> p n v q")
+                )
+            st[("g2", un)] = g2
+
+        def quant_xn(un):
+            g2 = st.pop(("g2", un))
+            c2 = work.tile([P, NB * P], U32, name="c2", align_bytes=64)
+            s2t = work.tile([P, NB * P], U8, name="s2t", align_bytes=64)
+            nc.vector.quantize_mx(
+                out=c2[:].bitcast(FP8X4), scales=s2t[:], in_=g2[:].rearrange("p n v q -> p (n v q)")
+            )
+            st[("c2", un)] = (c2, s2t)
+
+        def s2(un):
+            t = un % TPB
+            c2, s2t = st.pop(("c2", un))
+            if t == 0:
+                m4_new = psm.tile([P, TPB, C], F32, name="m4")
+                st["m4"] = m4_new
+            m4 = st["m4"]
+            for n in range(NB):
+                nc.tensor.matmul_mx(
+                    out=m4[:, t, :],
+                    lhsT=c2[:, n * P : (n + 1) * P].bitcast(FP8X4),
+                    lhsT_scale=s2t[:, n * P : (n + 1) * P],
+                    rhs=cc[:].bitcast(FP8X4),
+                    rhs_scale=cs[:],
+                    start=(n == 0),
+                    stop=(n == NB - 1),
+                )
+
+        def ep_exp(first, t0, nt):
+            m4 = st["m4"]
+            q = epi.tile([P, nt, C], F32, name="q")
+            z = small.tile([P, 4], F32, name="z")
+            for t in range(nt):
+                nc.scalar.activation(
+                    out=q[:, t, :], in_=m4[:, t0 + t, :], func=ACT.Exp, scale=5.0, accum_out=z[:, t : t + 1]
+                )
+            st[("q", first)] = (q, z)
+
+        def ep_a(first, nt):
+            q, z = st.pop(("q", first))
+            rows = slice(first * P, (first + nt) * P)
+            rz = small.tile([P, 4], F32, name="rz")
+            nc.vector.reciprocal(out=rz[:, 0:nt], in_=z[:, 0:nt])
+            pa = epi.tile([P, nt, C], F32, name="pa")
+            nc.vector.tensor_tensor(
+                out=pa[:], in0=q[:], in1=rz[:, 0:nt].unsqueeze(2).to_broadcast([P, nt, C]), op=ALU.mult
+            )
+            nc.sync.dma_start(out=out_0[rows, :].rearrange("(t p) c -> p t c", p=P), in_=pa[:])
+            st[("pa", first)] = pa
+
+        def ep_b(first, nt):
+            pa = st.pop(("pa", first))
+            tiles = slice(first, first + nt)
+            t1 = epi.tile([P, nt, C], F32, name="t1")
+            nc.vector.scalar_tensor_tensor(
+                out=t1[:], in0=pa[:], scalar=EPS, in1=u[:, tiles, :], op0=ALU.add, op1=ALU.mult
+            )
+            t2 = epi.tile([P, nt, C], F32, name="t2")
+            nc.vector.scalar_tensor_tensor(
+                out=t2[:], in0=pa[:], scalar=-(1.0 + EPS), in1=um1[:, tiles, :], op0=ALU.add, op1=ALU.mult
+            )
+            den = epi.tile([P, nt, C], F32, name="den")
+            nc.gpsimd.tensor_tensor(out=den[:], in0=t1[:], in1=t2[:], op=ALU.add)
+            st[("den", first)] = (t1, den)
+
+        def ep_c(first, nt):
+            t1, den = st.pop(("den", first))
+            rows = slice(first * P, (first + nt) * P)
+            rden = epi.tile([P, nt, C], F32, name="rden")
+            nc.vector.reciprocal(out=rden[:], in_=den[:])
+            mask = epi.tile([P, nt, C], F32, name="mask")
+            nc.gpsimd.tensor_tensor(out=mask[:], in0=t1[:], in1=rden[:], op=ALU.mult)
+            nc.sync.dma_start(out=out_1[rows, :].rearrange("(t p) c -> p t c", p=P), in_=mask[:])
+
+        def prep_and_load(k):
+            prep_x(k)
+            if k + 8 < NB * NVB:
+                load_x(k + 8)
+
         w_sb = const.tile([P, 4, S], BF16, name="w_sb")
         nc.sync.dma_start(out=w_sb[:], in_=W.rearrange("(a p) t -> p a t", p=P))
         for k in range(8):
@@ -79,11 +234,20 @@ def tile_cluster_assigner_pa_t_kernel(tc, x, cluster_emb, W, b, noise, out_0, ou
         nc.scalar.dma_start(out=b_bc[:], in_=b.partition_broadcast(P))
         u = const.tile([P, UNITS, C], BF16, name="u")
         nc.gpsimd.dma_start(out=u[:], in_=noise.rearrange("(t p) c -> p t c", p=P))
+        um1 = const.tile([P, UNITS, C], F32, name="um1")
 
         ident = const.tile([P, P], BF16, name="ident")
         make_identity(nc, ident[:])
         mhalf = const.tile([P, 4], F32, name="mhalf")
         nc.vector.memset(mhalf[:], -0.5)
+
+        junk0 = work.tile([P, D], BF16, name="junk")
+        ssc = small.tile([P, 4], F32, name="ss")
+        nc.scalar.activation(out=junk0[:], in_=ce[:], func=ACT.Square, accum_out=ssc[:, 0:1])
+        rc = const.tile([P, 1], F32, name="rc")
+        rsqrt_clamped(rc[:, 0:1], ssc[:, 0:1], 1)
+
+        prep_and_load(0)
 
         gw = const.tile([P, 4, P, 4], BF16, name="gw", align_bytes=64)
         for h in range(2):
@@ -95,7 +259,7 @@ def tile_cluster_assigner_pa_t_kernel(tc, x, cluster_emb, W, b, noise, out_0, ou
                         w_sb[:, 2 * h + a2, :].rearrange("p (q j) -> p j q", j=4)[:, j, :],
                         ident[:],
                     )
-            nc.vector.tensor_copy(
+            nc.scalar.copy(
                 out=gw[:, 2 * h : 2 * h + 2, :, :], in_=wt[:].rearrange("p a j d -> p a d j")
             )
         wc = const.tile([P, D], U32, name="wc", align_bytes=64)
@@ -104,151 +268,74 @@ def tile_cluster_assigner_pa_t_kernel(tc, x, cluster_emb, W, b, noise, out_0, ou
             out=wc[:].bitcast(FP8X4), scales=ws[:], in_=gw[:].rearrange("p a d j -> p (a d j)")
         )
 
-        def rsqrt_clamped(out, in_, width):
-            cl = small.tile([P, 4], F32, name="cl")
-            nc.gpsimd.tensor_scalar(
-                out=cl[:, 0:width], in0=in_, scalar1=3.0e38, scalar2=1e-24, op0=ALU.min, op1=ALU.max
-            )
-            nc.gpsimd.tensor_tensor(out=out, in0=cl[:, 0:width], in1=mhalf[:, 0:width], op=ALU.pow)
-
-        junk0 = work.tile([P, D], BF16, name="junk")
-        ssc = small.tile([P, 4], F32, name="ss")
-        nc.scalar.activation(out=junk0[:], in_=ce[:], func=ACT.Square, accum_out=ssc[:, 0:1])
-        rc = small.tile([P, 4], F32, name="rn")
-        rsqrt_clamped(rc[:, 0:1], ssc[:, 0:1], 1)
         cn = const.tile([P, D], BF16, name="cn")
-        nc.vector.tensor_scalar(out=cn[:], in0=ce[:], scalar1=rc[:, 0:1], scalar2=None, op0=ALU.mult)
-        ct = pst.tile([P, 2, 4, P], BF16, name="xt")
-        for t in range(4):
-            nc.tensor.transpose(ct[:, 0, t, :], cn[:, t * P : (t + 1) * P], ident[:])
         gc = const.tile([P, C, 4], BF16, name="gc", align_bytes=64)
-        nc.vector.tensor_copy(out=gc[:], in_=ct[:, 0, :, :].rearrange("p t c -> p c t"))
         cc = const.tile([P, C], U32, name="cc", align_bytes=64)
         cs = const.tile([P, C], U8, name="cs", align_bytes=64)
-        nc.vector.quantize_mx(
-            out=cc[:].bitcast(FP8X4), scales=cs[:], in_=gc[:].rearrange("p c t -> p (c t)")
-        )
 
-        um1 = const.tile([P, UNITS, C], F32, name="um1")
-        nc.gpsimd.tensor_scalar(
-            out=um1[:], in0=u[:], scalar1=1.0, scalar2=-1.0, op0=ALU.mult, op1=ALU.add
-        )
+        s1(0, 0)
+        prep_and_load(1)
+        s1(0, 1)
+        add_square(0, 0)
+        prep_and_load(2)
+        s1(0, 2)
+        add_square(0, 1)
+        prep_and_load(3)
+        s1(0, 3)
+        add_square(0, 2)
+        add_square(0, 3)
+        rnorm(0)
+        prep_and_load(4)
 
-        state = {}
-
-        def stage_a(un):
-            vb, t = divmod(un, TPB)
-            xe = xep.tile([P, NB, D], F32, name="xe")
-            ss = small.tile([P, 4], F32, name="ss")
-            for n in range(NB):
-                codes, scales = xcodes[vb * NB + n]
-                e = pse.tile([P, D], F32, name="e")
-                nc.tensor.matmul_mx(
-                    out=e[:],
-                    lhsT=codes[:, t * P : (t + 1) * P].bitcast(FP8X4),
-                    lhsT_scale=scales[:, t * P : (t + 1) * P],
-                    rhs=wc[:].bitcast(FP8X4),
-                    rhs_scale=ws[:],
-                    start=True,
-                    stop=True,
+        last_first = UNITS - TPB
+        for j in range(UNITS + 4):
+            done = j - 4
+            if 0 <= done < last_first and done % TPB == TPB - 1:
+                ep_exp(done - (TPB - 1), 0, TPB)
+            if last_first <= done < UNITS:
+                ep_exp(done, done % TPB, 1)
+            if 1 <= j < UNITS:
+                for n in range(NB):
+                    add_square(j, n)
+                rnorm(j)
+            if j % TPB == 0 and j < UNITS:
+                tiles = slice(j, j + TPB)
+                nc.gpsimd.tensor_scalar(
+                    out=um1[:, tiles, :], in0=u[:, tiles, :], scalar1=1.0, scalar2=-1.0, op0=ALU.mult, op1=ALU.add
                 )
-                nc.vector.tensor_tensor(out=xe[:, n, :], in0=e[:], in1=b_bc[:], op=ALU.add)
-                junk = work.tile([P, D], BF16, name="junk")
-                nc.scalar.activation(
-                    out=junk[:], in_=xe[:, n, :], func=ACT.Square, accum_out=ss[:, n : n + 1]
+            if j == 0:
+                nc.vector.tensor_scalar(out=cn[:], in0=ce[:], scalar1=rc[:, 0:1], scalar2=None, op0=ALU.mult)
+            if 0 <= j - 1 < UNITS:
+                scale(j - 1)
+            if j == 1:
+                nc.scalar.copy(out=gc[:], in_=st.pop("ct")[:, 0, :, :].rearrange("p t c -> p c t"))
+            if 0 <= j - 2 < UNITS:
+                copy_out(j - 2)
+            if j == 2:
+                nc.vector.quantize_mx(
+                    out=cc[:].bitcast(FP8X4), scales=cs[:], in_=gc[:].rearrange("p c t -> p (c t)")
                 )
-            rn = small.tile([P, 4], F32, name="rn")
-            rsqrt_clamped(rn[:], ss[:], 4)
-            state[un] = (xe, rn)
-
-        def stage_b(un):
-            vb, t = divmod(un, TPB)
-            xe, rn = state.pop(un)
-            xn = work.tile([P, NB, D], BF16, name="xn")
-            for n in range(NB):
-                if n % 2 == 0:
-                    nc.vector.tensor_scalar(
-                        out=xn[:, n, :], in0=xe[:, n, :], scalar1=rn[:, n : n + 1], scalar2=None, op0=ALU.mult
-                    )
-                else:
-                    nc.scalar.activation(
-                        out=xn[:, n, :], in_=xe[:, n, :], func=ACT.Copy, scale=rn[:, n : n + 1]
-                    )
-            g2 = work.tile([P, NB, P, 4], BF16, name="g2", align_bytes=64)
-            for h in range(2):
-                xt = pst.tile([P, 2, 4, P], BF16, name="xt")
-                for n2 in range(2):
-                    for q in range(4):
-                        nc.tensor.transpose(
-                            xt[:, n2, q, :], xn[:, 2 * h + n2, q * P : (q + 1) * P], ident[:]
-                        )
-                nc.scalar.copy(
-                    out=g2[:, 2 * h : 2 * h + 2, :, :], in_=xt[:].rearrange("p n q v -> p n v q")
-                )
-            c2 = work.tile([P, NB * P], U32, name="c2", align_bytes=64)
-            s2 = work.tile([P, NB * P], U8, name="s2", align_bytes=64)
-            nc.vector.quantize_mx(
-                out=c2[:].bitcast(FP8X4), scales=s2[:], in_=g2[:].rearrange("p n v q -> p (n v q)")
-            )
-            if t == 0:
-                m4_new = psm.tile([P, TPB, C], F32, name="m4")
-                state["m4"] = m4_new
-            m4 = state["m4"]
-            for n in range(NB):
-                nc.tensor.matmul_mx(
-                    out=m4[:, t, :],
-                    lhsT=c2[:, n * P : (n + 1) * P].bitcast(FP8X4),
-                    lhsT_scale=s2[:, n * P : (n + 1) * P],
-                    rhs=cc[:].bitcast(FP8X4),
-                    rhs_scale=cs[:],
-                    start=(n == 0),
-                    stop=(n == NB - 1),
-                )
-            if vb == NVB - 1:
-                epilogue(m4, un, t, 1)
-            elif t == TPB - 1:
-                epilogue(m4, un - t, 0, TPB)
-
-        def epilogue(m4, first, t0, nt):
-            tiles = slice(first, first + nt)
-            rows = slice(first * P, (first + nt) * P)
-            q = epi.tile([P, nt, C], F32, name="q")
-            z = small.tile([P, 4], F32, name="z")
-            for t in range(nt):
-                nc.scalar.activation(
-                    out=q[:, t, :], in_=m4[:, t0 + t, :], func=ACT.Exp, scale=5.0, accum_out=z[:, t : t + 1]
-                )
-            rz = small.tile([P, 4], F32, name="rz")
-            nc.vector.reciprocal(out=rz[:, 0:nt], in_=z[:, 0:nt])
-            pa = epi.tile([P, nt, C], F32, name="pa")
-            nc.vector.tensor_tensor(
-                out=pa[:], in0=q[:], in1=rz[:, 0:nt].unsqueeze(2).to_broadcast([P, nt, C]), op=ALU.mult
-            )
-            nc.sync.dma_start(out=out_0[rows, :].rearrange("(t p) c -> p t c", p=P), in_=pa[:])
-            t1 = epi.tile([P, nt, C], F32, name="t1")
-            nc.vector.scalar_tensor_tensor(
-                out=t1[:], in0=pa[:], scalar=EPS, in1=u[:, tiles, :], op0=ALU.add, op1=ALU.mult
-            )
-            t2 = epi.tile([P, nt, C], F32, name="t2")
-            nc.vector.scalar_tensor_tensor(
-                out=t2[:], in0=pa[:], scalar=-(1.0 + EPS), in1=um1[:, tiles, :], op0=ALU.add, op1=ALU.mult
-            )
-            den = epi.tile([P, nt, C], F32, name="den")
-            nc.gpsimd.tensor_tensor(out=den[:], in0=t1[:], in1=t2[:], op=ALU.add)
-            rden = epi.tile([P, nt, C], F32, name="rden")
-            nc.vector.reciprocal(out=rden[:], in_=den[:])
-            mask = epi.tile([P, nt, C], F32, name="mask")
-            nc.gpsimd.tensor_tensor(out=mask[:], in0=t1[:], in1=rden[:], op=ALU.mult)
-            nc.sync.dma_start(out=out_1[rows, :].rearrange("(t p) c -> p t c", p=P), in_=mask[:])
-
-        for k in range(4):
-            prep_x(k)
-        for un in range(UNITS + 1):
-            if un < UNITS:
-                if un + 8 < UNITS:
-                    load_x(un + 8)
-                if un + 4 < UNITS:
-                    prep_x(un + 4)
-                stage_a(un)
-            if un >= 1:
-                stage_b(un - 1)
+            if 0 <= j - 3 < UNITS:
+                quant_xn(j - 3)
+            if j + 1 < UNITS:
+                for n in range(NB):
+                    s1(j + 1, n)
+            if 0 <= j - 3 < UNITS:
+                s2(j - 3)
+            if j == 0:
+                ct = pst.tile([P, 2, 4, P], BF16, name="xt")
+                for t in range(4):
+                    nc.tensor.transpose(ct[:, 0, t, :], cn[:, t * P : (t + 1) * P], ident[:])
+                st["ct"] = ct
+            if 0 <= j - 1 < UNITS:
+                transposes(j - 1)
+            if j + 5 < NB * NVB:
+                prep_and_load(j + 5)
+            for lag, phase in ((0, ep_a), (1, ep_b), (2, ep_c)):
+                d2 = done - lag
+                if 0 <= d2 < last_first and d2 % TPB == TPB - 1:
+                    phase(d2 - (TPB - 1), TPB)
+            if last_first <= done < UNITS:
+                ep_a(done, 1)
+                ep_b(done, 1)
+                ep_c(done, 1)

@@ -31,7 +31,7 @@ def tile_cluster_assigner_pa_t_kernel(tc, x, cluster_emb, W, b, noise, out_0, ou
     with ExitStack() as ctx:
         const = ctx.enter_context(tc.tile_pool(name="const", bufs=1))
         rawp = ctx.enter_context(tc.tile_pool(name="rawp", bufs=8))
-        xgp = ctx.enter_context(tc.tile_pool(name="xgp", bufs=2))
+        xgp = ctx.enter_context(tc.tile_pool(name="xgp", bufs=3))
         xcp = ctx.enter_context(tc.tile_pool(name="xcp", bufs=10))
         xep = ctx.enter_context(tc.tile_pool(name="xep", bufs=3))
         work = ctx.enter_context(tc.tile_pool(name="work", bufs=2))
@@ -55,13 +55,19 @@ def tile_cluster_assigner_pa_t_kernel(tc, x, cluster_emb, W, b, noise, out_0, ou
             )
             raws[k] = raw
 
-        def prep_x(k):
+        def regroup_x(k):
             raw = raws.pop(k)
             g = xgp.tile([P, VB, 4], BF16, name="xg", align_bytes=64)
             nc.vector.tensor_copy(
                 out=g[:].rearrange("p (c i) t -> p c t i", i=4),
                 in_=raw[:].rearrange("p t (c i) -> p c t i", i=4),
             )
+            st[("xg", k)] = g
+            if k + 8 < NB * NVB:
+                load_x(k + 8)
+
+        def quant_x(k):
+            g = st.pop(("xg", k))
             codes = xcp.tile([P, VB], U32, name="xcodes", align_bytes=64)
             scales = xcp.tile([P, VB], U8, name="xscales", align_bytes=64)
             nc.vector.quantize_mx(
@@ -93,7 +99,7 @@ def tile_cluster_assigner_pa_t_kernel(tc, x, cluster_emb, W, b, noise, out_0, ou
             )
             st[("e", un, n)] = e
 
-        def add_square(un, n):
+        def add_bias(un, n):
             if n == 0:
                 xe_new = xep.tile([P, NB, D], F32, name="xe")
                 ss_new = small.tile([P, 4], F32, name="ss")
@@ -102,6 +108,9 @@ def tile_cluster_assigner_pa_t_kernel(tc, x, cluster_emb, W, b, noise, out_0, ou
             xe = st[("xe", un)]
             e = st.pop(("e", un, n))
             nc.vector.tensor_tensor(out=xe[:, n, :], in0=e[:], in1=b_bc[:], op=ALU.add)
+
+        def square(un, n):
+            xe = st[("xe", un)]
             junk = work.tile([P, D], BF16, name="junk")
             nc.scalar.activation(
                 out=junk[:], in_=xe[:, n, :], func=ACT.Square, accum_out=st[("ss", un)][:, n : n + 1]
@@ -112,19 +121,24 @@ def tile_cluster_assigner_pa_t_kernel(tc, x, cluster_emb, W, b, noise, out_0, ou
             rsqrt_clamped(rn[:], st.pop(("ss", un))[:], 4)
             st[("rn", un)] = rn
 
-        def scale(un):
-            xe = st.pop(("xe", un))
-            rn = st.pop(("rn", un))
+        def scale_g(un):
+            xe = st[("xe", un)]
+            rn = st[("rn", un)]
             xn = work.tile([P, NB, D], BF16, name="xn")
             for n in range(2):
-                nc.vector.tensor_scalar(
-                    out=xn[:, n, :], in0=xe[:, n, :], scalar1=rn[:, n : n + 1], scalar2=None, op0=ALU.mult
+                nc.gpsimd.tensor_scalar(
+                    out=xn[:, n, :], in0=xe[:, n, :], scalar1=rn[:, n : n + 1], scalar2=0.0, op0=ALU.mult, op1=ALU.add
                 )
+            st[("xn", un)] = xn
+
+        def scale_s(un):
+            xe = st.pop(("xe", un))
+            rn = st.pop(("rn", un))
+            xn = st[("xn", un)]
             for n in range(2, NB):
                 nc.scalar.activation(
                     out=xn[:, n, :], in_=xe[:, n, :], func=ACT.Copy, scale=rn[:, n : n + 1]
                 )
-            st[("xn", un)] = xn
 
         def transposes(un):
             xn = st.pop(("xn", un))
@@ -137,14 +151,15 @@ def tile_cluster_assigner_pa_t_kernel(tc, x, cluster_emb, W, b, noise, out_0, ou
                         )
                 st[("xt", un, h)] = xt
 
-        def copy_out(un):
-            g2 = work.tile([P, NB, P, 4], BF16, name="g2", align_bytes=64)
-            for h in range(2):
-                xt = st.pop(("xt", un, h))
-                nc.scalar.copy(
-                    out=g2[:, 2 * h : 2 * h + 2, :, :], in_=xt[:].rearrange("p n q v -> p n v q")
-                )
-            st[("g2", un)] = g2
+        def copy_out(un, h):
+            if h == 0:
+                g2_new = work.tile([P, NB, P, 4], BF16, name="g2", align_bytes=64)
+                st[("g2", un)] = g2_new
+            g2 = st[("g2", un)]
+            xt = st.pop(("xt", un, h))
+            nc.scalar.copy(
+                out=g2[:, 2 * h : 2 * h + 2, :, :], in_=xt[:].rearrange("p n q v -> p n v q")
+            )
 
         def quant_xn(un):
             g2 = st.pop(("g2", un))
@@ -183,15 +198,19 @@ def tile_cluster_assigner_pa_t_kernel(tc, x, cluster_emb, W, b, noise, out_0, ou
                 )
             st[("q", first)] = (q, z)
 
-        def ep_a(first, nt):
-            q, z = st.pop(("q", first))
-            rows = slice(first * P, (first + nt) * P)
+        def ep_rz(first, nt):
+            q, z = st[("q", first)]
             rz = small.tile([P, 4], F32, name="rz")
             nc.vector.reciprocal(out=rz[:, 0:nt], in_=z[:, 0:nt])
+            st[("rz", first)] = rz
+
+        def ep_pa(first, nt):
+            q, z = st.pop(("q", first))
+            rz = st.pop(("rz", first))
+            rows = slice(first * P, (first + nt) * P)
             pa = epi.tile([P, nt, C], F32, name="pa")
-            nc.vector.tensor_tensor(
-                out=pa[:], in0=q[:], in1=rz[:, 0:nt].unsqueeze(2).to_broadcast([P, nt, C]), op=ALU.mult
-            )
+            for t in range(nt):
+                nc.scalar.activation(out=pa[:, t, :], in_=q[:, t, :], func=ACT.Copy, scale=rz[:, t : t + 1])
             nc.sync.dma_start(out=out_0[rows, :].rearrange("(t p) c -> p t c", p=P), in_=pa[:])
             st[("pa", first)] = pa
 
@@ -202,12 +221,10 @@ def tile_cluster_assigner_pa_t_kernel(tc, x, cluster_emb, W, b, noise, out_0, ou
             nc.vector.scalar_tensor_tensor(
                 out=t1[:], in0=pa[:], scalar=EPS, in1=u[:, tiles, :], op0=ALU.add, op1=ALU.mult
             )
-            t2 = epi.tile([P, nt, C], F32, name="t2")
-            nc.vector.scalar_tensor_tensor(
-                out=t2[:], in0=pa[:], scalar=-(1.0 + EPS), in1=um1[:, tiles, :], op0=ALU.add, op1=ALU.mult
-            )
+            d1 = epi.tile([P, nt, C], F32, name="d1")
+            nc.gpsimd.tensor_tensor(out=d1[:], in0=pa[:], in1=w1[:, tiles, :], op=ALU.mult)
             den = epi.tile([P, nt, C], F32, name="den")
-            nc.gpsimd.tensor_tensor(out=den[:], in0=t1[:], in1=t2[:], op=ALU.add)
+            nc.gpsimd.tensor_tensor(out=den[:], in0=d1[:], in1=w2[:, tiles, :], op=ALU.add)
             st[("den", first)] = (t1, den)
 
         def ep_c(first, nt):
@@ -219,11 +236,6 @@ def tile_cluster_assigner_pa_t_kernel(tc, x, cluster_emb, W, b, noise, out_0, ou
             nc.gpsimd.tensor_tensor(out=mask[:], in0=t1[:], in1=rden[:], op=ALU.mult)
             nc.sync.dma_start(out=out_1[rows, :].rearrange("(t p) c -> p t c", p=P), in_=mask[:])
 
-        def prep_and_load(k):
-            prep_x(k)
-            if k + 8 < NB * NVB:
-                load_x(k + 8)
-
         w_sb = const.tile([P, 4, S], BF16, name="w_sb")
         nc.sync.dma_start(out=w_sb[:], in_=W.rearrange("(a p) t -> p a t", p=P))
         for k in range(8):
@@ -234,7 +246,8 @@ def tile_cluster_assigner_pa_t_kernel(tc, x, cluster_emb, W, b, noise, out_0, ou
         nc.scalar.dma_start(out=b_bc[:], in_=b.partition_broadcast(P))
         u = const.tile([P, UNITS, C], BF16, name="u")
         nc.gpsimd.dma_start(out=u[:], in_=noise.rearrange("(t p) c -> p t c", p=P))
-        um1 = const.tile([P, UNITS, C], F32, name="um1")
+        w1 = const.tile([P, UNITS, C], F32, name="w1")
+        w2 = const.tile([P, UNITS, C], F32, name="w2")
 
         ident = const.tile([P, P], BF16, name="ident")
         make_identity(nc, ident[:])
@@ -247,7 +260,8 @@ def tile_cluster_assigner_pa_t_kernel(tc, x, cluster_emb, W, b, noise, out_0, ou
         rc = const.tile([P, 1], F32, name="rc")
         rsqrt_clamped(rc[:, 0:1], ssc[:, 0:1], 1)
 
-        prep_and_load(0)
+        regroup_x(0)
+        quant_x(0)
 
         gw = const.tile([P, 4, P, 4], BF16, name="gw", align_bytes=64)
         for h in range(2):
@@ -274,43 +288,74 @@ def tile_cluster_assigner_pa_t_kernel(tc, x, cluster_emb, W, b, noise, out_0, ou
         cs = const.tile([P, C], U8, name="cs", align_bytes=64)
 
         s1(0, 0)
-        prep_and_load(1)
+        regroup_x(1)
+        regroup_x(2)
+        quant_x(1)
         s1(0, 1)
-        add_square(0, 0)
-        prep_and_load(2)
+        add_bias(0, 0)
+        square(0, 0)
+        regroup_x(3)
+        quant_x(2)
         s1(0, 2)
-        add_square(0, 1)
-        prep_and_load(3)
+        add_bias(0, 1)
+        square(0, 1)
+        regroup_x(4)
+        quant_x(3)
         s1(0, 3)
-        add_square(0, 2)
-        add_square(0, 3)
+        add_bias(0, 2)
+        square(0, 2)
+        add_bias(0, 3)
+        square(0, 3)
         rnorm(0)
-        prep_and_load(4)
+        regroup_x(5)
+        quant_x(4)
 
         last_first = UNITS - TPB
+
+        def block_end(d):
+            return 0 <= d < last_first and d % TPB == TPB - 1
+
         for j in range(UNITS + 4):
             done = j - 4
-            if 0 <= done < last_first and done % TPB == TPB - 1:
+            live = 1 <= j < UNITS
+            if block_end(done):
                 ep_exp(done - (TPB - 1), 0, TPB)
             if last_first <= done < UNITS:
                 ep_exp(done, done % TPB, 1)
-            if 1 <= j < UNITS:
-                for n in range(NB):
-                    add_square(j, n)
-                rnorm(j)
-            if j % TPB == 0 and j < UNITS:
-                tiles = slice(j, j + TPB)
-                nc.gpsimd.tensor_scalar(
-                    out=um1[:, tiles, :], in0=u[:, tiles, :], scalar1=1.0, scalar2=-1.0, op0=ALU.mult, op1=ALU.add
-                )
-            if j == 0:
-                nc.vector.tensor_scalar(out=cn[:], in0=ce[:], scalar1=rc[:, 0:1], scalar2=None, op0=ALU.mult)
+            if block_end(done - 1):
+                ep_pa(done - 1 - (TPB - 1), TPB)
             if 0 <= j - 1 < UNITS:
-                scale(j - 1)
+                scale_g(j - 1)
+            if live:
+                add_bias(j, 0)
+                add_bias(j, 1)
             if j == 1:
                 nc.scalar.copy(out=gc[:], in_=st.pop("ct")[:, 0, :, :].rearrange("p t c -> p c t"))
             if 0 <= j - 2 < UNITS:
-                copy_out(j - 2)
+                copy_out(j - 2, 0)
+            if live:
+                square(j, 0)
+                square(j, 1)
+                add_bias(j, 2)
+                add_bias(j, 3)
+            if 0 <= j - 2 < UNITS:
+                copy_out(j - 2, 1)
+            if live:
+                square(j, 2)
+                square(j, 3)
+                rnorm(j)
+            if 0 <= j - 1 < UNITS:
+                scale_s(j - 1)
+            if j % TPB == 0 and j < UNITS:
+                tiles = slice(j, j + TPB)
+                nc.gpsimd.tensor_scalar(
+                    out=w1[:, tiles, :], in0=u[:, tiles, :], scalar1=2.0, scalar2=-1.0, op0=ALU.mult, op1=ALU.add
+                )
+                nc.gpsimd.tensor_scalar(
+                    out=w2[:, tiles, :], in0=u[:, tiles, :], scalar1=-1.0, scalar2=1.0 + EPS, op0=ALU.mult, op1=ALU.add
+                )
+            if j == 0:
+                nc.vector.tensor_scalar(out=cn[:], in0=ce[:], scalar1=rc[:, 0:1], scalar2=None, op0=ALU.mult)
             if j == 2:
                 nc.vector.quantize_mx(
                     out=cc[:].bitcast(FP8X4), scales=cs[:], in_=gc[:].rearrange("p c t -> p (c t)")
@@ -329,13 +374,18 @@ def tile_cluster_assigner_pa_t_kernel(tc, x, cluster_emb, W, b, noise, out_0, ou
                 st["ct"] = ct
             if 0 <= j - 1 < UNITS:
                 transposes(j - 1)
+            if j + 6 < NB * NVB:
+                regroup_x(j + 6)
             if j + 5 < NB * NVB:
-                prep_and_load(j + 5)
-            for lag, phase in ((0, ep_a), (1, ep_b), (2, ep_c)):
-                d2 = done - lag
-                if 0 <= d2 < last_first and d2 % TPB == TPB - 1:
-                    phase(d2 - (TPB - 1), TPB)
+                quant_x(j + 5)
+            if block_end(done):
+                ep_rz(done - (TPB - 1), TPB)
+            if block_end(done - 1):
+                ep_b(done - 1 - (TPB - 1), TPB)
+            if block_end(done - 2):
+                ep_c(done - 2 - (TPB - 1), TPB)
             if last_first <= done < UNITS:
-                ep_a(done, 1)
+                ep_rz(done, 1)
+                ep_pa(done, 1)
                 ep_b(done, 1)
                 ep_c(done, 1)

@@ -10,6 +10,7 @@ U8 = mybir.dt.uint8
 FP8X4 = mybir.dt.float8_e4m3fn_x4
 ALU = mybir.AluOpType
 ACT = mybir.ActivationFunctionType
+AX = mybir.AxisListType
 
 P = 128
 NB = 4
@@ -20,7 +21,7 @@ D = 512
 VB = 512
 NVB = V // VB
 TPB = VB // P
-UNITS = V // P
+UNITS = NB * NVB
 EPS = 1e-10
 
 FLOPS = 2 * NB * V * S * D + 2 * NB * V * D * C
@@ -30,20 +31,21 @@ def tile_cluster_assigner_pa_t_kernel(tc, x, cluster_emb, W, b, noise, out_0, ou
     nc = tc.nc
     with ExitStack() as ctx:
         const = ctx.enter_context(tc.tile_pool(name="const", bufs=1))
-        rawp = ctx.enter_context(tc.tile_pool(name="rawp", bufs=8))
+        rawp = ctx.enter_context(tc.tile_pool(name="rawp", bufs=5))
         xgp = ctx.enter_context(tc.tile_pool(name="xgp", bufs=3))
-        xcp = ctx.enter_context(tc.tile_pool(name="xcp", bufs=10))
-        xep = ctx.enter_context(tc.tile_pool(name="xep", bufs=3))
+        xcp = ctx.enter_context(tc.tile_pool(name="xcp", bufs=4))
+        xep = ctx.enter_context(tc.tile_pool(name="xep", bufs=5))
+        sqp = ctx.enter_context(tc.tile_pool(name="sqp", bufs=2))
         work = ctx.enter_context(tc.tile_pool(name="work", bufs=2))
+        c2p = ctx.enter_context(tc.tile_pool(name="c2p", bufs=7))
         small = ctx.enter_context(tc.tile_pool(name="small", bufs=4))
         epi = ctx.enter_context(tc.tile_pool(name="epi", bufs=2))
         pse = ctx.enter_context(tc.psum_pool(name="pse", bufs=4))
-        pst = ctx.enter_context(tc.psum_pool(name="pst", bufs=3))
+        psa = ctx.enter_context(tc.psum_pool(name="psa", bufs=2))
+        psr = ctx.enter_context(tc.psum_pool(name="psr", bufs=1))
         psm = ctx.enter_context(tc.psum_pool(name="psm", bufs=1))
         ctx.enter_context(tc.manual_schedule())
 
-        raws = {}
-        xcodes = {}
         st = {}
 
         def load_x(k):
@@ -53,29 +55,27 @@ def tile_cluster_assigner_pa_t_kernel(tc, x, cluster_emb, W, b, noise, out_0, ou
                 out=raw[:],
                 in_=x[n, :, vb * VB : (vb + 1) * VB].rearrange("(p j) w -> p j w", j=4),
             )
-            raws[k] = raw
+            st[("raw", k)] = raw
 
         def regroup_x(k):
-            raw = raws.pop(k)
+            raw = st.pop(("raw", k))
             g = xgp.tile([P, VB, 4], BF16, name="xg", align_bytes=64)
             nc.vector.tensor_copy(
                 out=g[:].rearrange("p (c i) t -> p c t i", i=4),
                 in_=raw[:].rearrange("p t (c i) -> p c t i", i=4),
             )
             st[("xg", k)] = g
-            if k + 8 < NB * NVB:
-                load_x(k + 8)
+            if k + 5 < UNITS:
+                load_x(k + 5)
 
         def quant_x(k):
             g = st.pop(("xg", k))
             codes = xcp.tile([P, VB], U32, name="xcodes", align_bytes=64)
             scales = xcp.tile([P, VB], U8, name="xscales", align_bytes=64)
             nc.vector.quantize_mx(
-                out=codes[:].bitcast(FP8X4),
-                scales=scales[:],
-                in_=g[:].rearrange("p w t -> p (w t)"),
+                out=codes[:].bitcast(FP8X4), scales=scales[:], in_=g[:].rearrange("p w t -> p (w t)")
             )
-            xcodes[k] = (codes, scales)
+            st[("xc", k)] = (codes, scales)
 
         def rsqrt_clamped(out, in_, width):
             cl = small.tile([P, 4], F32, name="cl")
@@ -84,173 +84,180 @@ def tile_cluster_assigner_pa_t_kernel(tc, x, cluster_emb, W, b, noise, out_0, ou
             )
             nc.gpsimd.tensor_tensor(out=out, in0=cl[:, 0:width], in1=mhalf[:, 0:width], op=ALU.pow)
 
-        def s1(un, n):
-            vb, t = divmod(un, TPB)
-            codes, scales = xcodes[vb * NB + n]
-            e = pse.tile([P, D], F32, name="e")
-            nc.tensor.matmul_mx(
-                out=e[:],
-                lhsT=codes[:, t * P : (t + 1) * P].bitcast(FP8X4),
-                lhsT_scale=scales[:, t * P : (t + 1) * P],
-                rhs=wc[:].bitcast(FP8X4),
-                rhs_scale=ws[:],
-                start=True,
-                stop=True,
-            )
-            st[("e", un, n)] = e
-
-        def add_bias(un, n):
-            if n == 0:
-                xe_new = xep.tile([P, NB, D], F32, name="xe")
-                ss_new = small.tile([P, 4], F32, name="ss")
-                st[("xe", un)] = xe_new
-                st[("ss", un)] = ss_new
-            xe = st[("xe", un)]
-            e = st.pop(("e", un, n))
-            nc.vector.tensor_tensor(out=xe[:, n, :], in0=e[:], in1=b_bc[:], op=ALU.add)
-
-        def square(un, n):
-            xe = st[("xe", un)]
-            junk = work.tile([P, D], BF16, name="junk")
-            nc.scalar.activation(
-                out=junk[:], in_=xe[:, n, :], func=ACT.Square, accum_out=st[("ss", un)][:, n : n + 1]
-            )
-
-        def rnorm(un):
-            rn = small.tile([P, 4], F32, name="rn")
-            rsqrt_clamped(rn[:], st.pop(("ss", un))[:], 4)
-            st[("rn", un)] = rn
-
-        def scale_g(un):
-            xe = st[("xe", un)]
-            rn = st[("rn", un)]
-            xn = work.tile([P, NB, D], BF16, name="xn")
-            for n in range(2):
-                nc.gpsimd.tensor_scalar(
-                    out=xn[:, n, :], in0=xe[:, n, :], scalar1=rn[:, n : n + 1], scalar2=0.0, op0=ALU.mult, op1=ALU.add
-                )
-            st[("xn", un)] = xn
-
-        def scale_s(un):
-            xe = st.pop(("xe", un))
-            rn = st.pop(("rn", un))
-            xn = st[("xn", un)]
-            for n in range(2, NB):
-                nc.scalar.activation(
-                    out=xn[:, n, :], in_=xe[:, n, :], func=ACT.Copy, scale=rn[:, n : n + 1]
-                )
-
-        def transposes(un):
-            xn = st.pop(("xn", un))
-            for h in range(2):
-                xt = pst.tile([P, 2, 4, P], BF16, name="xt")
-                for n2 in range(2):
-                    for q in range(4):
-                        nc.tensor.transpose(
-                            xt[:, n2, q, :], xn[:, 2 * h + n2, q * P : (q + 1) * P], ident[:]
-                        )
-                st[("xt", un, h)] = xt
-
-        def copy_out(un, h):
-            if h == 0:
-                g2_new = work.tile([P, NB, P, 4], BF16, name="g2", align_bytes=64)
-                st[("g2", un)] = g2_new
-            g2 = st[("g2", un)]
-            xt = st.pop(("xt", un, h))
-            nc.scalar.copy(
-                out=g2[:, 2 * h : 2 * h + 2, :, :], in_=xt[:].rearrange("p n q v -> p n v q")
-            )
-
-        def quant_xn(un):
-            g2 = st.pop(("g2", un))
-            c2 = work.tile([P, NB * P], U32, name="c2", align_bytes=64)
-            s2t = work.tile([P, NB * P], U8, name="s2t", align_bytes=64)
-            nc.vector.quantize_mx(
-                out=c2[:].bitcast(FP8X4), scales=s2t[:], in_=g2[:].rearrange("p n v q -> p (n v q)")
-            )
-            st[("c2", un)] = (c2, s2t)
-
-        def s2(un):
-            t = un % TPB
-            c2, s2t = st.pop(("c2", un))
-            if t == 0:
-                m4_new = psm.tile([P, TPB, C], F32, name="m4")
-                st["m4"] = m4_new
-            m4 = st["m4"]
-            for n in range(NB):
+        def s1(k):
+            codes, scales = st.pop(("xc", k))
+            for jj in range(4):
+                e = pse.tile([P, VB], F32, name="e")
                 nc.tensor.matmul_mx(
-                    out=m4[:, t, :],
-                    lhsT=c2[:, n * P : (n + 1) * P].bitcast(FP8X4),
-                    lhsT_scale=s2t[:, n * P : (n + 1) * P],
-                    rhs=cc[:].bitcast(FP8X4),
-                    rhs_scale=cs[:],
-                    start=(n == 0),
-                    stop=(n == NB - 1),
+                    out=e[:],
+                    lhsT=wc[:, jj * P : (jj + 1) * P].bitcast(FP8X4),
+                    lhsT_scale=ws[:, jj * P : (jj + 1) * P],
+                    rhs=codes[:].bitcast(FP8X4),
+                    rhs_scale=scales[:],
+                    start=True,
+                    stop=True,
                 )
+                st[("e", k, jj)] = e
 
-        def ep_exp(first, t0, nt):
-            m4 = st["m4"]
-            q = epi.tile([P, nt, C], F32, name="q")
-            z = small.tile([P, 4], F32, name="z")
-            for t in range(nt):
+        def evac(k):
+            xe = xep.tile([P, 4, VB], F32, name="xe")
+            for jj in range(4):
+                e = st.pop(("e", k, jj))
                 nc.scalar.activation(
-                    out=q[:, t, :], in_=m4[:, t0 + t, :], func=ACT.Exp, scale=5.0, accum_out=z[:, t : t + 1]
+                    out=xe[:, jj, :], in_=e[:], func=ACT.Identity, bias=bcol[:, jj : jj + 1]
                 )
-            st[("q", first)] = (q, z)
+            st[("xe", k)] = xe
 
-        def ep_rz(first, nt):
-            q, z = st[("q", first)]
+        def square(k):
+            xe = st[("xe", k)]
+            sq = sqp.tile([P, 4, VB], F32, name="sq")
+            half = VB // 2
+            for h in range(2):
+                cols = slice(h * half, (h + 1) * half)
+                nc.scalar.activation(out=sq[:, :, cols], in_=xe[:, :, cols], func=ACT.Square)
+            st[("sq", k)] = sq
+
+        def tacc(k):
+            sq = st.pop(("sq", k))
+            acc = psa.tile([P, TPB, P], F32, name="acc")
+            for i in range(TPB):
+                for jj in range(4):
+                    nc.tensor.matmul(
+                        out=acc[:, i, :],
+                        lhsT=sq[:, jj, i * P : (i + 1) * P],
+                        rhs=identf[:],
+                        is_transpose=True,
+                        start=(jj == 0),
+                        stop=(jj == 3),
+                    )
+            st[("acc", k)] = acc
+
+        def reduce_norm(k):
+            acc = st.pop(("acc", k))
+            ss = small.tile([P, 4], F32, name="ss")
+            nc.vector.tensor_reduce(out=ss[:], in_=acc[:], axis=AX.X, op=ALU.add)
+            rn = small.tile([P, 4], F32, name="rn")
+            rsqrt_clamped(rn[:], ss[:], 4)
+            st[("rn", k)] = rn
+
+        def spread(k):
+            rn = st.pop(("rn", k))
+            rnb = psr.tile([P, VB], F32, name="rnb")
+            for i in range(TPB):
+                nc.tensor.matmul(
+                    out=rnb[:, i * P : (i + 1) * P],
+                    lhsT=rn[:, i : i + 1].to_broadcast([P, P]),
+                    rhs=identf[:],
+                    start=True,
+                    stop=True,
+                )
+            st[("rnb", k)] = rnb
+
+        def final(k):
+            xe = st.pop(("xe", k))
+            rnb = st.pop(("rnb", k))
+            g2 = work.tile([P, VB, 4], BF16, name="g2", align_bytes=64)
+            nc.vector.tensor_tensor(
+                out=g2[:],
+                in0=xe[:].rearrange("p j v -> p v j"),
+                in1=rnb[:].unsqueeze(2).to_broadcast([P, VB, 4]),
+                op=ALU.mult,
+            )
+            st[("g2", k)] = g2
+
+        def quant_xn(k):
+            g2 = st.pop(("g2", k))
+            c2 = c2p.tile([P, VB], U32, name="c2", align_bytes=64)
+            s2t = c2p.tile([P, VB], U8, name="s2t", align_bytes=64)
+            nc.vector.quantize_mx(
+                out=c2[:].bitcast(FP8X4), scales=s2t[:], in_=g2[:].rearrange("p v j -> p (v j)")
+            )
+            st[("c2", k)] = (c2, s2t)
+
+        def s2(vb):
+            m4 = psm.tile([P, TPB, C], F32, name="m4")
+            ops = [st.pop(("c2", vb * NB + n)) for n in range(NB)]
+            for i in range(TPB):
+                for n in range(NB):
+                    c2, s2t = ops[n]
+                    nc.tensor.matmul_mx(
+                        out=m4[:, i, :],
+                        lhsT=c2[:, i * P : (i + 1) * P].bitcast(FP8X4),
+                        lhsT_scale=s2t[:, i * P : (i + 1) * P],
+                        rhs=cc[:].bitcast(FP8X4),
+                        rhs_scale=cs[:],
+                        start=(n == 0),
+                        stop=(n == NB - 1),
+                    )
+            st[("m4", vb)] = m4
+
+        def ep_exp(vb):
+            m4 = st.pop(("m4", vb))
+            q = epi.tile([P, TPB, C], F32, name="q")
+            z = small.tile([P, 4], F32, name="z")
+            for t in range(TPB):
+                nc.scalar.activation(
+                    out=q[:, t, :], in_=m4[:, t, :], func=ACT.Exp, scale=5.0, accum_out=z[:, t : t + 1]
+                )
+            st[("q", vb)] = (q, z)
+
+        def ep_rz(vb):
+            q, z = st[("q", vb)]
             rz = small.tile([P, 4], F32, name="rz")
-            nc.vector.reciprocal(out=rz[:, 0:nt], in_=z[:, 0:nt])
-            st[("rz", first)] = rz
+            nc.vector.reciprocal(out=rz[:], in_=z[:])
+            st[("rz", vb)] = rz
 
-        def ep_pa(first, nt):
-            q, z = st.pop(("q", first))
-            rz = st.pop(("rz", first))
-            rows = slice(first * P, (first + nt) * P)
-            pa = epi.tile([P, nt, C], F32, name="pa")
-            for t in range(nt):
+        def ep_pa(vb):
+            q, z = st.pop(("q", vb))
+            rz = st.pop(("rz", vb))
+            rows = slice(vb * VB, (vb + 1) * VB)
+            pa = epi.tile([P, TPB, C], F32, name="pa")
+            for t in range(TPB):
                 nc.scalar.activation(out=pa[:, t, :], in_=q[:, t, :], func=ACT.Copy, scale=rz[:, t : t + 1])
             nc.sync.dma_start(out=out_0[rows, :].rearrange("(t p) c -> p t c", p=P), in_=pa[:])
-            st[("pa", first)] = pa
+            st[("pa", vb)] = pa
 
-        def ep_b(first, nt):
-            pa = st.pop(("pa", first))
-            tiles = slice(first, first + nt)
-            t1 = epi.tile([P, nt, C], F32, name="t1")
+        def ep_b(vb, eng):
+            pa = st.pop(("pa", vb))
+            tiles = slice(vb * TPB, (vb + 1) * TPB)
+            t1 = epi.tile([P, TPB, C], F32, name="t1")
             nc.vector.scalar_tensor_tensor(
                 out=t1[:], in0=pa[:], scalar=EPS, in1=u[:, tiles, :], op0=ALU.add, op1=ALU.mult
             )
-            d1 = epi.tile([P, nt, C], F32, name="d1")
-            nc.gpsimd.tensor_tensor(out=d1[:], in0=pa[:], in1=w1[:, tiles, :], op=ALU.mult)
-            den = epi.tile([P, nt, C], F32, name="den")
-            nc.gpsimd.tensor_tensor(out=den[:], in0=d1[:], in1=w2[:, tiles, :], op=ALU.add)
-            st[("den", first)] = (t1, den)
+            t2 = epi.tile([P, TPB, C], F32, name="t2")
+            nc.vector.scalar_tensor_tensor(
+                out=t2[:], in0=pa[:], scalar=-(1.0 + EPS), in1=um1[:, tiles, :], op0=ALU.add, op1=ALU.mult
+            )
+            den = epi.tile([P, TPB, C], F32, name="den")
+            eng.tensor_tensor(out=den[:], in0=t1[:], in1=t2[:], op=ALU.add)
+            st[("den", vb)] = (t1, den)
 
-        def ep_c(first, nt):
-            t1, den = st.pop(("den", first))
-            rows = slice(first * P, (first + nt) * P)
-            rden = epi.tile([P, nt, C], F32, name="rden")
+        def ep_c(vb, eng):
+            t1, den = st.pop(("den", vb))
+            rows = slice(vb * VB, (vb + 1) * VB)
+            rden = epi.tile([P, TPB, C], F32, name="rden")
             nc.vector.reciprocal(out=rden[:], in_=den[:])
-            mask = epi.tile([P, nt, C], F32, name="mask")
-            nc.gpsimd.tensor_tensor(out=mask[:], in0=t1[:], in1=rden[:], op=ALU.mult)
+            mask = epi.tile([P, TPB, C], F32, name="mask")
+            eng.tensor_tensor(out=mask[:], in0=t1[:], in1=rden[:], op=ALU.mult)
             nc.sync.dma_start(out=out_1[rows, :].rearrange("(t p) c -> p t c", p=P), in_=mask[:])
 
         w_sb = const.tile([P, 4, S], BF16, name="w_sb")
         nc.sync.dma_start(out=w_sb[:], in_=W.rearrange("(a p) t -> p a t", p=P))
-        for k in range(8):
+        for k in range(5):
             load_x(k)
+        zb = const.tile([P, P], BF16, name="zb")
+        nc.vector.memset(zb[:], 0.0)
+        nc.scalar.dma_start(out=zb[0:4, :], in_=b.rearrange("(j p) -> j p", p=P))
         ce = const.tile([P, D], BF16, name="ce")
         nc.scalar.dma_start(out=ce[:], in_=cluster_emb)
-        b_bc = const.tile([P, D], BF16, name="b_bc")
-        nc.scalar.dma_start(out=b_bc[:], in_=b.partition_broadcast(P))
-        u = const.tile([P, UNITS, C], BF16, name="u")
+        u = const.tile([P, V // P, C], BF16, name="u")
         nc.gpsimd.dma_start(out=u[:], in_=noise.rearrange("(t p) c -> p t c", p=P))
-        w1 = const.tile([P, UNITS, C], F32, name="w1")
-        w2 = const.tile([P, UNITS, C], F32, name="w2")
+        um1 = const.tile([P, V // P, C], F32, name="um1")
 
         ident = const.tile([P, P], BF16, name="ident")
         make_identity(nc, ident[:])
+        identf = const.tile([P, P], F32, name="identf")
+        make_identity(nc, identf[:])
         mhalf = const.tile([P, 4], F32, name="mhalf")
         nc.vector.memset(mhalf[:], -0.5)
 
@@ -265,7 +272,7 @@ def tile_cluster_assigner_pa_t_kernel(tc, x, cluster_emb, W, b, noise, out_0, ou
 
         gw = const.tile([P, 4, P, 4], BF16, name="gw", align_bytes=64)
         for h in range(2):
-            wt = pst.tile([P, 2, 4, P], BF16, name="xt")
+            wt = pse.tile([P, 2, 4, P], BF16, name="e")
             for a2 in range(2):
                 for j in range(4):
                     nc.tensor.transpose(
@@ -281,111 +288,77 @@ def tile_cluster_assigner_pa_t_kernel(tc, x, cluster_emb, W, b, noise, out_0, ou
         nc.vector.quantize_mx(
             out=wc[:].bitcast(FP8X4), scales=ws[:], in_=gw[:].rearrange("p a d j -> p (a d j)")
         )
+        bt = pse.tile([P, P], BF16, name="e")
+        nc.tensor.transpose(bt[:], zb[:], ident[:])
+        bcol = const.tile([P, 4], F32, name="bcol")
+        nc.vector.tensor_copy(out=bcol[:], in_=bt[:, 0:4])
 
         cn = const.tile([P, D], BF16, name="cn")
         gc = const.tile([P, C, 4], BF16, name="gc", align_bytes=64)
         cc = const.tile([P, C], U32, name="cc", align_bytes=64)
         cs = const.tile([P, C], U8, name="cs", align_bytes=64)
 
-        s1(0, 0)
+        s1(0)
         regroup_x(1)
         regroup_x(2)
         quant_x(1)
-        s1(0, 1)
-        add_bias(0, 0)
-        square(0, 0)
-        regroup_x(3)
-        quant_x(2)
-        s1(0, 2)
-        add_bias(0, 1)
-        square(0, 1)
-        regroup_x(4)
-        quant_x(3)
-        s1(0, 3)
-        add_bias(0, 2)
-        square(0, 2)
-        add_bias(0, 3)
-        square(0, 3)
-        rnorm(0)
-        regroup_x(5)
-        quant_x(4)
-
-        last_first = UNITS - TPB
-
-        def block_end(d):
-            return 0 <= d < last_first and d % TPB == TPB - 1
 
         for j in range(UNITS + 4):
-            done = j - 4
-            live = 1 <= j < UNITS
-            if block_end(done):
-                ep_exp(done - (TPB - 1), 0, TPB)
-            if last_first <= done < UNITS:
-                ep_exp(done, done % TPB, 1)
-            if block_end(done - 1):
-                ep_pa(done - 1 - (TPB - 1), TPB)
-            if 0 <= j - 1 < UNITS:
-                scale_g(j - 1)
-            if live:
-                add_bias(j, 0)
-                add_bias(j, 1)
+            vb_s2, r_s2 = divmod(j - 7, NB)
+            vb_ex, r_ex = divmod(j - 8, NB)
+            vb_pa, r_pa = divmod(j - 9, NB)
+            vb_c, r_c = divmod(j - 10, NB)
+            if r_ex == 0 and 0 <= vb_ex < NVB:
+                ep_exp(vb_ex)
+            if r_pa == 0 and 0 <= vb_pa < NVB:
+                ep_pa(vb_pa)
+            if j < UNITS:
+                evac(j)
+                square(j)
+            if j % NB == 0 and j < UNITS:
+                tiles = slice(j, j + NB)
+                nc.scalar.activation(out=um1[:, tiles, :], in_=u[:, tiles, :], func=ACT.Copy, bias=-1.0)
             if j == 1:
                 nc.scalar.copy(out=gc[:], in_=st.pop("ct")[:, 0, :, :].rearrange("p t c -> p c t"))
             if 0 <= j - 2 < UNITS:
-                copy_out(j - 2, 0)
-            if live:
-                square(j, 0)
-                square(j, 1)
-                add_bias(j, 2)
-                add_bias(j, 3)
-            if 0 <= j - 2 < UNITS:
-                copy_out(j - 2, 1)
-            if live:
-                square(j, 2)
-                square(j, 3)
-                rnorm(j)
-            if 0 <= j - 1 < UNITS:
-                scale_s(j - 1)
-            if j % TPB == 0 and j < UNITS:
-                tiles = slice(j, j + TPB)
-                nc.gpsimd.tensor_scalar(
-                    out=w1[:, tiles, :], in0=u[:, tiles, :], scalar1=2.0, scalar2=-1.0, op0=ALU.mult, op1=ALU.add
-                )
-                nc.gpsimd.tensor_scalar(
-                    out=w2[:, tiles, :], in0=u[:, tiles, :], scalar1=-1.0, scalar2=1.0 + EPS, op0=ALU.mult, op1=ALU.add
-                )
+                reduce_norm(j - 2)
+            if 0 <= j - 3 < UNITS:
+                final(j - 3)
             if j == 0:
                 nc.vector.tensor_scalar(out=cn[:], in0=ce[:], scalar1=rc[:, 0:1], scalar2=None, op0=ALU.mult)
+            if r_s2 == 0 and 0 <= vb_s2 < NVB:
+                s2(vb_s2)
+            if 0 <= j - 1 < UNITS:
+                tacc(j - 1)
+            if j + 1 < UNITS:
+                s1(j + 1)
+            if 0 <= j - 2 < UNITS:
+                spread(j - 2)
+            if j == 0:
+                ct = pse.tile([P, 2, 4, P], BF16, name="e")
+                for t in range(4):
+                    nc.tensor.transpose(ct[:, 0, t, :], cn[:, t * P : (t + 1) * P], ident[:])
+                st["ct"] = ct
+            if j + 3 < UNITS:
+                regroup_x(j + 3)
             if j == 2:
                 nc.vector.quantize_mx(
                     out=cc[:].bitcast(FP8X4), scales=cs[:], in_=gc[:].rearrange("p c t -> p (c t)")
                 )
             if 0 <= j - 3 < UNITS:
                 quant_xn(j - 3)
-            if j + 1 < UNITS:
-                for n in range(NB):
-                    s1(j + 1, n)
-            if 0 <= j - 3 < UNITS:
-                s2(j - 3)
-            if j == 0:
-                ct = pst.tile([P, 2, 4, P], BF16, name="xt")
-                for t in range(4):
-                    nc.tensor.transpose(ct[:, 0, t, :], cn[:, t * P : (t + 1) * P], ident[:])
-                st["ct"] = ct
-            if 0 <= j - 1 < UNITS:
-                transposes(j - 1)
-            if j + 6 < NB * NVB:
-                regroup_x(j + 6)
-            if j + 5 < NB * NVB:
-                quant_x(j + 5)
-            if block_end(done):
-                ep_rz(done - (TPB - 1), TPB)
-            if block_end(done - 1):
-                ep_b(done - 1 - (TPB - 1), TPB)
-            if block_end(done - 2):
-                ep_c(done - 2 - (TPB - 1), TPB)
-            if last_first <= done < UNITS:
-                ep_rz(done, 1)
-                ep_pa(done, 1)
-                ep_b(done, 1)
-                ep_c(done, 1)
+            if j + 2 < UNITS:
+                quant_x(j + 2)
+            if r_ex == 0 and 0 <= vb_ex < NVB:
+                ep_rz(vb_ex)
+            if r_pa == 0 and 0 <= vb_pa < NVB:
+                ep_b(vb_pa, nc.gpsimd)
+            if r_c == 0 and 0 <= vb_c < NVB:
+                ep_c(vb_c, nc.gpsimd)
+
+        last = NVB - 1
+        ep_exp(last)
+        ep_rz(last)
+        ep_pa(last)
+        ep_b(last, nc.vector)
+        ep_c(last, nc.vector)

@@ -140,17 +140,18 @@ def tile_cluster_assigner_pa_t_kernel(tc, x, cluster_emb, W, b, noise, out_0, ou
             rsqrt_clamped(rn[:], ss[:], 4)
             st[("rn", k)] = rn
 
-        def spread(k):
+        def repeat_rn(k):
             rn = st.pop(("rn", k))
+            rep = work.tile([P, TPB, P], F32, name="rep")
+            for i in range(TPB):
+                nc.scalar.activation(out=rep[:, i, :], in_=ones[:], func=ACT.Copy, scale=rn[:, i : i + 1])
+            st[("rep", k)] = rep
+
+        def spread(k):
+            rep = st.pop(("rep", k))
             rnb = psr.tile([P, VB], F32, name="rnb")
             for i in range(TPB):
-                nc.tensor.matmul(
-                    out=rnb[:, i * P : (i + 1) * P],
-                    lhsT=rn[:, i : i + 1].to_broadcast([P, P]),
-                    rhs=identf[:],
-                    start=True,
-                    stop=True,
-                )
+                nc.tensor.transpose(rnb[:, i * P : (i + 1) * P], rep[:, i, :], identf[:])
             st[("rnb", k)] = rnb
 
         def final(k):
@@ -260,6 +261,8 @@ def tile_cluster_assigner_pa_t_kernel(tc, x, cluster_emb, W, b, noise, out_0, ou
         make_identity(nc, identf[:])
         mhalf = const.tile([P, 4], F32, name="mhalf")
         nc.vector.memset(mhalf[:], -0.5)
+        ones = const.tile([P, P], F32, name="ones")
+        nc.vector.memset(ones[:], 1.0)
 
         junk0 = work.tile([P, D], BF16, name="junk")
         ssc = small.tile([P, 4], F32, name="ss")
@@ -322,14 +325,15 @@ def tile_cluster_assigner_pa_t_kernel(tc, x, cluster_emb, W, b, noise, out_0, ou
                 nc.scalar.copy(out=gc[:], in_=st.pop("ct")[:, 0, :, :].rearrange("p t c -> p c t"))
             if 0 <= j - 2 < UNITS:
                 reduce_norm(j - 2)
+                repeat_rn(j - 2)
             if 0 <= j - 3 < UNITS:
                 final(j - 3)
             if j == 0:
                 nc.vector.tensor_scalar(out=cn[:], in0=ce[:], scalar1=rc[:, 0:1], scalar2=None, op0=ALU.mult)
-            if r_s2 == 0 and 0 <= vb_s2 < NVB:
-                s2(vb_s2)
             if 0 <= j - 1 < UNITS:
                 tacc(j - 1)
+            if r_s2 == 0 and 0 <= vb_s2 < NVB:
+                s2(vb_s2)
             if j + 1 < UNITS:
                 s1(j + 1)
             if 0 <= j - 2 < UNITS:

@@ -140,18 +140,18 @@ def tile_cluster_assigner_pa_t_kernel(tc, x, cluster_emb, W, b, noise, out_0, ou
             rsqrt_clamped(rn[:], ss[:], 4)
             st[("rn", k)] = rn
 
-        def repeat_rn(k):
-            rn = st.pop(("rn", k))
-            rep = work.tile([P, TPB, P], F32, name="rep")
-            for i in range(TPB):
-                nc.scalar.activation(out=rep[:, i, :], in_=ones[:], func=ACT.Copy, scale=rn[:, i : i + 1])
-            st[("rep", k)] = rep
-
         def spread(k):
-            rep = st.pop(("rep", k))
+            rn = st.pop(("rn", k))
             rnb = psr.tile([P, VB], F32, name="rnb")
             for i in range(TPB):
-                nc.tensor.transpose(rnb[:, i * P : (i + 1) * P], rep[:, i, :], identf[:])
+                nc.tensor.matmul(
+                    out=rnb[:, i * P : (i + 1) * P],
+                    lhsT=rn[:, i : i + 1].to_broadcast([P, P]),
+                    rhs=identf[:],
+                    is_transpose=True,
+                    start=True,
+                    stop=True,
+                )
             st[("rnb", k)] = rnb
 
         def final(k):
@@ -261,8 +261,6 @@ def tile_cluster_assigner_pa_t_kernel(tc, x, cluster_emb, W, b, noise, out_0, ou
         make_identity(nc, identf[:])
         mhalf = const.tile([P, 4], F32, name="mhalf")
         nc.vector.memset(mhalf[:], -0.5)
-        ones = const.tile([P, P], F32, name="ones")
-        nc.vector.memset(ones[:], 1.0)
 
         junk0 = work.tile([P, D], BF16, name="junk")
         ssc = small.tile([P, 4], F32, name="ss")
@@ -325,7 +323,6 @@ def tile_cluster_assigner_pa_t_kernel(tc, x, cluster_emb, W, b, noise, out_0, ou
                 nc.scalar.copy(out=gc[:], in_=st.pop("ct")[:, 0, :, :].rearrange("p t c -> p c t"))
             if 0 <= j - 2 < UNITS:
                 reduce_norm(j - 2)
-                repeat_rn(j - 2)
             if 0 <= j - 3 < UNITS:
                 final(j - 3)
             if j == 0:

@@ -10,7 +10,6 @@ U8 = mybir.dt.uint8
 FP8X4 = mybir.dt.float8_e4m3fn_x4
 ALU = mybir.AluOpType
 ACT = mybir.ActivationFunctionType
-AX = mybir.AxisListType
 
 P = 128
 NB = 4
@@ -108,34 +107,30 @@ def tile_cluster_assigner_pa_t_kernel(tc, x, cluster_emb, W, b, noise, out_0, ou
                 )
             st[("xe", k)] = xe
 
-        def square(k):
+        def turn(k, i):
             xe = st[("xe", k)]
-            sq = sqp.tile([P, 4, VB], F32, name="sq")
-            half = VB // 2
-            for h in range(2):
-                cols = slice(h * half, (h + 1) * half)
-                nc.scalar.activation(out=sq[:, :, cols], in_=xe[:, :, cols], func=ACT.Square)
-            st[("sq", k)] = sq
+            xt = psa.tile([P, 4, P], F32, name="xt")
+            for jj in range(4):
+                nc.tensor.transpose(xt[:, jj, :], xe[:, jj, i * P : (i + 1) * P], identf[:])
+            st[("xt", k, i)] = xt
 
-        def tacc(k):
-            sq = st.pop(("sq", k))
-            acc = psa.tile([P, TPB, P], F32, name="acc")
-            for i in range(TPB):
-                for jj in range(4):
-                    nc.tensor.matmul(
-                        out=acc[:, i, :],
-                        lhsT=sq[:, jj, i * P : (i + 1) * P],
-                        rhs=identf[:],
-                        is_transpose=True,
-                        start=(jj == 0),
-                        stop=(jj == 3),
-                    )
-            st[("acc", k)] = acc
+        def square_sum(k, i, ss):
+            xt = st.pop(("xt", k, i))
+            junk = sqp.tile([P, D], BF16, name="sq")
+            nc.scalar.activation(
+                out=junk[:], in_=xt[:].rearrange("p j d -> p (j d)"), func=ACT.Square, accum_out=ss[:, i : i + 1]
+            )
 
-        def reduce_norm(k):
-            acc = st.pop(("acc", k))
+        def norms(k):
             ss = small.tile([P, 4], F32, name="ss")
-            nc.vector.tensor_reduce(out=ss[:], in_=acc[:], axis=AX.X, op=ALU.add)
+            turn(k, 0)
+            turn(k, 1)
+            square_sum(k, 0, ss)
+            turn(k, 2)
+            square_sum(k, 1, ss)
+            turn(k, 3)
+            square_sum(k, 2, ss)
+            square_sum(k, 3, ss)
             rn = small.tile([P, 4], F32, name="rn")
             rsqrt_clamped(rn[:], ss[:], 4)
             st[("rn", k)] = rn
@@ -315,20 +310,17 @@ def tile_cluster_assigner_pa_t_kernel(tc, x, cluster_emb, W, b, noise, out_0, ou
                 ep_pa(vb_pa)
             if j < UNITS:
                 evac(j)
-                square(j)
             if j % NB == 0 and j < UNITS:
                 tiles = slice(j, j + NB)
                 nc.scalar.activation(out=um1[:, tiles, :], in_=u[:, tiles, :], func=ACT.Copy, bias=-1.0)
             if j == 1:
                 nc.scalar.copy(out=gc[:], in_=st.pop("ct")[:, 0, :, :].rearrange("p t c -> p c t"))
-            if 0 <= j - 2 < UNITS:
-                reduce_norm(j - 2)
             if 0 <= j - 3 < UNITS:
                 final(j - 3)
             if j == 0:
                 nc.vector.tensor_scalar(out=cn[:], in0=ce[:], scalar1=rc[:, 0:1], scalar2=None, op0=ALU.mult)
             if 0 <= j - 1 < UNITS:
-                tacc(j - 1)
+                norms(j - 1)
             if r_s2 == 0 and 0 <= vb_s2 < NVB:
                 s2(vb_s2)
             if j + 1 < UNITS:

@@ -31,14 +31,15 @@ def tile_cluster_assigner_pa_t_kernel(tc, x, cluster_emb, W, b, noise, out_0, ou
     with ExitStack() as ctx:
         const = ctx.enter_context(tc.tile_pool(name="const", bufs=1))
         rawp = ctx.enter_context(tc.tile_pool(name="rawp", bufs=5))
-        xgp = ctx.enter_context(tc.tile_pool(name="xgp", bufs=3))
-        xcp = ctx.enter_context(tc.tile_pool(name="xcp", bufs=4))
+        xgp = ctx.enter_context(tc.tile_pool(name="xgp", bufs=4))
+        xcp = ctx.enter_context(tc.tile_pool(name="xcp", bufs=5))
         xep = ctx.enter_context(tc.tile_pool(name="xep", bufs=5))
         sqp = ctx.enter_context(tc.tile_pool(name="sqp", bufs=2))
         work = ctx.enter_context(tc.tile_pool(name="work", bufs=2))
-        c2p = ctx.enter_context(tc.tile_pool(name="c2p", bufs=7))
-        small = ctx.enter_context(tc.tile_pool(name="small", bufs=4))
+        c2p = ctx.enter_context(tc.tile_pool(name="c2p", bufs=12))
+        small = ctx.enter_context(tc.tile_pool(name="small", bufs=6))
         epi = ctx.enter_context(tc.tile_pool(name="epi", bufs=2))
+        epi4 = ctx.enter_context(tc.tile_pool(name="epi4", bufs=4))
         pse = ctx.enter_context(tc.psum_pool(name="pse", bufs=4))
         psa = ctx.enter_context(tc.psum_pool(name="psa", bufs=2))
         psr = ctx.enter_context(tc.psum_pool(name="psr", bufs=1))
@@ -83,9 +84,9 @@ def tile_cluster_assigner_pa_t_kernel(tc, x, cluster_emb, W, b, noise, out_0, ou
             )
             nc.gpsimd.tensor_tensor(out=out, in0=cl[:, 0:width], in1=mhalf[:, 0:width], op=ALU.pow)
 
-        def s1(k):
-            codes, scales = st.pop(("xc", k))
-            for jj in range(4):
+        def s1(k, half):
+            codes, scales = st[("xc", k)]
+            for jj in (2 * half, 2 * half + 1):
                 e = pse.tile([P, VB], F32, name="e")
                 nc.tensor.matmul_mx(
                     out=e[:],
@@ -98,14 +99,16 @@ def tile_cluster_assigner_pa_t_kernel(tc, x, cluster_emb, W, b, noise, out_0, ou
                 )
                 st[("e", k, jj)] = e
 
-        def evac(k):
-            xe = xep.tile([P, 4, VB], F32, name="xe")
-            for jj in range(4):
+        def evac(k, half):
+            if half == 0:
+                xe = xep.tile([P, 4, VB], F32, name="xe")
+                st[("xe", k)] = xe
+            xe = st[("xe", k)]
+            for jj in (2 * half, 2 * half + 1):
                 e = st.pop(("e", k, jj))
                 nc.scalar.activation(
                     out=xe[:, jj, :], in_=e[:], func=ACT.Identity, bias=bcol[:, jj : jj + 1]
                 )
-            st[("xe", k)] = xe
 
         def turn(k, i):
             xe = st[("xe", k)]
@@ -114,7 +117,10 @@ def tile_cluster_assigner_pa_t_kernel(tc, x, cluster_emb, W, b, noise, out_0, ou
                 nc.tensor.transpose(xt[:, jj, :], xe[:, jj, i * P : (i + 1) * P], identf[:])
             st[("xt", k, i)] = xt
 
-        def square_sum(k, i, ss):
+        def square_sum(k, i):
+            if i == 0:
+                st[("ss", k)] = small.tile([P, 4], F32, name="ss")
+            ss = st[("ss", k)]
             xt = st.pop(("xt", k, i))
             junk = sqp.tile([P, D], BF16, name="sq")
             nc.scalar.activation(
@@ -122,22 +128,14 @@ def tile_cluster_assigner_pa_t_kernel(tc, x, cluster_emb, W, b, noise, out_0, ou
             )
 
         def norms(k):
-            ss = small.tile([P, 4], F32, name="ss")
-            turn(k, 0)
-            turn(k, 1)
-            square_sum(k, 0, ss)
-            turn(k, 2)
-            square_sum(k, 1, ss)
-            turn(k, 3)
-            square_sum(k, 2, ss)
-            square_sum(k, 3, ss)
+            ss = st.pop(("ss", k))
             rn = small.tile([P, 4], F32, name="rn")
             rsqrt_clamped(rn[:], ss[:], 4)
             st[("rn", k)] = rn
 
         def spread(k):
             rn = st.pop(("rn", k))
-            rnb = psr.tile([P, VB], F32, name="rnb")
+            rnb = psr.tile([P, VB], F32, name="bank")
             for i in range(TPB):
                 nc.tensor.matmul(
                     out=rnb[:, i * P : (i + 1) * P],
@@ -170,72 +168,71 @@ def tile_cluster_assigner_pa_t_kernel(tc, x, cluster_emb, W, b, noise, out_0, ou
             )
             st[("c2", k)] = (c2, s2t)
 
-        def s2(vb):
-            m4 = psm.tile([P, TPB, C], F32, name="m4")
-            ops = [st.pop(("c2", vb * NB + n)) for n in range(NB)]
-            for i in range(TPB):
-                for n in range(NB):
-                    c2, s2t = ops[n]
-                    nc.tensor.matmul_mx(
-                        out=m4[:, i, :],
-                        lhsT=c2[:, i * P : (i + 1) * P].bitcast(FP8X4),
-                        lhsT_scale=s2t[:, i * P : (i + 1) * P],
-                        rhs=cc[:].bitcast(FP8X4),
-                        rhs_scale=cs[:],
-                        start=(n == 0),
-                        stop=(n == NB - 1),
-                    )
-            st[("m4", vb)] = m4
-
-        def ep_exp(vb):
-            m4 = st.pop(("m4", vb))
-            q = epi.tile([P, TPB, C], F32, name="q")
-            z = small.tile([P, 4], F32, name="z")
-            for t in range(TPB):
-                nc.scalar.activation(
-                    out=q[:, t, :], in_=m4[:, t, :], func=ACT.Exp, scale=5.0, accum_out=z[:, t : t + 1]
+        def s2(vb, t):
+            if t == 0:
+                m4 = psm.tile([P, TPB, C], F32, name="m4")
+                st[("m4", vb)] = m4
+            m4 = st[("m4", vb)]
+            for n in range(NB):
+                c2, s2t = st[("c2", vb * NB + n)]
+                nc.tensor.matmul_mx(
+                    out=m4[:, t, :],
+                    lhsT=c2[:, t * P : (t + 1) * P].bitcast(FP8X4),
+                    lhsT_scale=s2t[:, t * P : (t + 1) * P],
+                    rhs=cc[:].bitcast(FP8X4),
+                    rhs_scale=cs[:],
+                    start=(n == 0),
+                    stop=(n == NB - 1),
                 )
-            st[("q", vb)] = (q, z)
 
-        def ep_rz(vb):
-            q, z = st[("q", vb)]
-            rz = small.tile([P, 4], F32, name="rz")
+        def ep_exp(vb, t):
+            m4 = st[("m4", vb)]
+            if t == 0:
+                st[("q", vb)] = epi.tile([P, TPB, C], F32, name="q")
+                st[("pa", vb)] = epi.tile([P, TPB, C], F32, name="pa")
+                st[("mask", vb)] = epi.tile([P, TPB, C], F32, name="mask")
+            q = st[("q", vb)]
+            z = small.tile([P, 1], F32, name="z")
+            nc.scalar.activation(out=q[:, t, :], in_=m4[:, t, :], func=ACT.Exp, scale=5.0, accum_out=z[:])
+            st[("z", vb, t)] = z
+
+        def ep_rz(vb, t):
+            z = st.pop(("z", vb, t))
+            rz = small.tile([P, 1], F32, name="rz")
             nc.vector.reciprocal(out=rz[:], in_=z[:])
-            st[("rz", vb)] = rz
+            st[("rz", vb, t)] = rz
 
-        def ep_pa(vb):
-            q, z = st.pop(("q", vb))
-            rz = st.pop(("rz", vb))
-            rows = slice(vb * VB, (vb + 1) * VB)
-            pa = epi.tile([P, TPB, C], F32, name="pa")
-            for t in range(TPB):
-                nc.scalar.activation(out=pa[:, t, :], in_=q[:, t, :], func=ACT.Copy, scale=rz[:, t : t + 1])
-            nc.sync.dma_start(out=out_0[rows, :].rearrange("(t p) c -> p t c", p=P), in_=pa[:])
-            st[("pa", vb)] = pa
+        def ep_pa(vb, t):
+            q = st[("q", vb)]
+            pa = st[("pa", vb)]
+            rz = st.pop(("rz", vb, t))
+            nc.scalar.activation(out=pa[:, t, :], in_=q[:, t, :], func=ACT.Copy, scale=rz[:])
+            if t == TPB - 1:
+                nc.sync.dma_start(out=out_0[vb * VB : (vb + 1) * VB, :].rearrange("(t p) c -> p t c", p=P), in_=pa[:])
 
-        def ep_b(vb, eng):
-            pa = st.pop(("pa", vb))
-            tiles = slice(vb * TPB, (vb + 1) * TPB)
-            t1 = epi.tile([P, TPB, C], F32, name="t1")
+        def ep_b(vb, t, eng):
+            pa = st[("pa", vb)]
+            tile = vb * TPB + t
+            t1 = epi4.tile([P, C], F32, name="t1")
             nc.vector.scalar_tensor_tensor(
-                out=t1[:], in0=pa[:], scalar=EPS, in1=u[:, tiles, :], op0=ALU.add, op1=ALU.mult
+                out=t1[:], in0=pa[:, t, :], scalar=EPS, in1=u[:, tile, :], op0=ALU.add, op1=ALU.mult
             )
-            t2 = epi.tile([P, TPB, C], F32, name="t2")
+            t2 = epi4.tile([P, C], F32, name="t2")
             nc.vector.scalar_tensor_tensor(
-                out=t2[:], in0=pa[:], scalar=-(1.0 + EPS), in1=um1[:, tiles, :], op0=ALU.add, op1=ALU.mult
+                out=t2[:], in0=pa[:, t, :], scalar=-(1.0 + EPS), in1=um1[:, tile, :], op0=ALU.add, op1=ALU.mult
             )
-            den = epi.tile([P, TPB, C], F32, name="den")
+            den = epi4.tile([P, C], F32, name="den")
             eng.tensor_tensor(out=den[:], in0=t1[:], in1=t2[:], op=ALU.add)
-            st[("den", vb)] = (t1, den)
+            st[("den", vb, t)] = (t1, den)
 
-        def ep_c(vb, eng):
-            t1, den = st.pop(("den", vb))
-            rows = slice(vb * VB, (vb + 1) * VB)
-            rden = epi.tile([P, TPB, C], F32, name="rden")
+        def ep_c(vb, t, eng):
+            t1, den = st.pop(("den", vb, t))
+            rden = epi4.tile([P, C], F32, name="rden")
             nc.vector.reciprocal(out=rden[:], in_=den[:])
-            mask = epi.tile([P, TPB, C], F32, name="mask")
-            eng.tensor_tensor(out=mask[:], in0=t1[:], in1=rden[:], op=ALU.mult)
-            nc.sync.dma_start(out=out_1[rows, :].rearrange("(t p) c -> p t c", p=P), in_=mask[:])
+            mask = st[("mask", vb)]
+            eng.tensor_tensor(out=mask[:, t, :], in0=t1[:], in1=rden[:], op=ALU.mult)
+            if t == TPB - 1:
+                nc.sync.dma_start(out=out_1[vb * VB : (vb + 1) * VB, :].rearrange("(t p) c -> p t c", p=P), in_=mask[:])
 
         w_sb = const.tile([P, 4, S], BF16, name="w_sb")
         nc.sync.dma_start(out=w_sb[:], in_=W.rearrange("(a p) t -> p a t", p=P))
@@ -294,64 +291,92 @@ def tile_cluster_assigner_pa_t_kernel(tc, x, cluster_emb, W, b, noise, out_0, ou
         cc = const.tile([P, C], U32, name="cc", align_bytes=64)
         cs = const.tile([P, C], U8, name="cs", align_bytes=64)
 
-        s1(0)
+        s1(0, 0)
+        s1(0, 1)
         regroup_x(1)
         regroup_x(2)
         quant_x(1)
+        regroup_x(3)
+        quant_x(2)
 
-        for j in range(UNITS + 4):
-            vb_s2, r_s2 = divmod(j - 7, NB)
-            vb_ex, r_ex = divmod(j - 8, NB)
-            vb_pa, r_pa = divmod(j - 9, NB)
-            vb_c, r_c = divmod(j - 10, NB)
-            if r_ex == 0 and 0 <= vb_ex < NVB:
-                ep_exp(vb_ex)
-            if r_pa == 0 and 0 <= vb_pa < NVB:
-                ep_pa(vb_pa)
+        def blk(e):
+            return divmod(e, TPB)
+
+        for j in range(UNITS + 8):
+            def on(k):
+                return 0 <= k < UNITS
+            def ep(k):
+                return 0 <= k < UNITS - TPB
+            if on(j - 3):
+                final(j - 3)
             if j < UNITS:
-                evac(j)
+                evac(j, 0)
+            if j + 1 < UNITS:
+                s1(j + 1, 0)
+            if on(j - 1):
+                square_sum(j - 1, 0)
+                square_sum(j - 1, 1)
+                turn(j - 1, 2)
+                turn(j - 1, 3)
+            if on(j - 2):
+                spread(j - 2)
+            if j < UNITS:
+                evac(j, 1)
+            if j + 1 < UNITS:
+                s1(j + 1, 1)
+            if ep(j - 7):
+                s2(*blk(j - 7))
+            if on(j - 1):
+                square_sum(j - 1, 2)
+                square_sum(j - 1, 3)
+            if j < UNITS:
+                turn(j, 0)
+                turn(j, 1)
+            if ep(j - 8):
+                ep_exp(*blk(j - 8))
+            if ep(j - 9):
+                ep_rz(*blk(j - 9))
+            if ep(j - 10):
+                ep_pa(*blk(j - 10))
             if j % NB == 0 and j < UNITS:
                 tiles = slice(j, j + NB)
                 nc.scalar.activation(out=um1[:, tiles, :], in_=u[:, tiles, :], func=ACT.Copy, bias=-1.0)
             if j == 1:
                 nc.scalar.copy(out=gc[:], in_=st.pop("ct")[:, 0, :, :].rearrange("p t c -> p c t"))
-            if 0 <= j - 3 < UNITS:
-                final(j - 3)
             if j == 0:
                 nc.vector.tensor_scalar(out=cn[:], in0=ce[:], scalar1=rc[:, 0:1], scalar2=None, op0=ALU.mult)
-            if 0 <= j - 1 < UNITS:
-                norms(j - 1)
-            if r_s2 == 0 and 0 <= vb_s2 < NVB:
-                s2(vb_s2)
-            if j + 1 < UNITS:
-                s1(j + 1)
-            if 0 <= j - 2 < UNITS:
-                spread(j - 2)
-            if j == 0:
-                ct = pse.tile([P, 2, 4, P], BF16, name="e")
+                ct = psm.tile([P, 2, 4, P], BF16, name="m4")
                 for t in range(4):
                     nc.tensor.transpose(ct[:, 0, t, :], cn[:, t * P : (t + 1) * P], ident[:])
                 st["ct"] = ct
-            if j + 3 < UNITS:
-                regroup_x(j + 3)
+            if j + 4 < UNITS:
+                regroup_x(j + 4)
             if j == 2:
                 nc.vector.quantize_mx(
                     out=cc[:].bitcast(FP8X4), scales=cs[:], in_=gc[:].rearrange("p c t -> p (c t)")
                 )
-            if 0 <= j - 3 < UNITS:
+            if on(j - 3):
                 quant_xn(j - 3)
-            if j + 2 < UNITS:
-                quant_x(j + 2)
-            if r_ex == 0 and 0 <= vb_ex < NVB:
-                ep_rz(vb_ex)
-            if r_pa == 0 and 0 <= vb_pa < NVB:
-                ep_b(vb_pa, nc.gpsimd)
-            if r_c == 0 and 0 <= vb_c < NVB:
-                ep_c(vb_c, nc.gpsimd)
+            if j + 3 < UNITS:
+                quant_x(j + 3)
+            if ep(j - 11):
+                ep_b(*blk(j - 11), nc.gpsimd)
+            if on(j - 1):
+                norms(j - 1)
+            if ep(j - 12):
+                ep_c(*blk(j - 12), nc.gpsimd)
+            if j == UNITS + 3:
+                for t in range(TPB):
+                    s2(NVB - 1, t)
 
         last = NVB - 1
-        ep_exp(last)
-        ep_rz(last)
-        ep_pa(last)
-        ep_b(last, nc.vector)
-        ep_c(last, nc.vector)
+        for t in range(TPB):
+            ep_exp(last, t)
+        for t in range(TPB):
+            ep_rz(last, t)
+        for t in range(TPB):
+            ep_pa(last, t)
+        for t in range(TPB):
+            ep_b(last, t, nc.vector)
+        for t in range(TPB):
+            ep_c(last, t, nc.vector)

@@ -152,9 +152,9 @@ def tile_cluster_assigner_pa_t_kernel(tc, x, cluster_emb, W, b, noise, out_0, ou
             rnb = st.pop(("rnb", k))
             g2 = work.tile([P, VB, 4], BF16, name="g2", align_bytes=64)
             nc.vector.tensor_tensor(
-                out=g2[:],
-                in0=xe[:].rearrange("p j v -> p v j"),
-                in1=rnb[:].unsqueeze(2).to_broadcast([P, VB, 4]),
+                out=g2[:].rearrange("p (c i) j -> p c j i", i=4),
+                in0=xe[:].rearrange("p j (c i) -> p c j i", i=4),
+                in1=rnb[:].rearrange("p (c i) -> p c i", i=4).unsqueeze(2).to_broadcast([P, VB // 4, 4, 4]),
                 op=ALU.mult,
             )
             st[("g2", k)] = g2

@@ -22,6 +22,8 @@ NVB = V // VB
 TPB = VB // P
 UNITS = NB * NVB
 EPS = 1e-10
+RAW = 5
+AHEAD = 7
 
 FLOPS = 2 * NB * V * S * D + 2 * NB * V * D * C
 
@@ -30,9 +32,9 @@ def tile_cluster_assigner_pa_t_kernel(tc, x, cluster_emb, W, b, noise, out_0, ou
     nc = tc.nc
     with ExitStack() as ctx:
         const = ctx.enter_context(tc.tile_pool(name="const", bufs=1))
-        rawp = ctx.enter_context(tc.tile_pool(name="rawp", bufs=5))
-        xgp = ctx.enter_context(tc.tile_pool(name="xgp", bufs=4))
-        xcp = ctx.enter_context(tc.tile_pool(name="xcp", bufs=5))
+        rawp = ctx.enter_context(tc.tile_pool(name="rawp", bufs=RAW))
+        xgp = ctx.enter_context(tc.tile_pool(name="xgp", bufs=3))
+        xcp = ctx.enter_context(tc.tile_pool(name="xcp", bufs=12))
         xep = ctx.enter_context(tc.tile_pool(name="xep", bufs=5))
         sqp = ctx.enter_context(tc.tile_pool(name="sqp", bufs=2))
         work = ctx.enter_context(tc.tile_pool(name="work", bufs=2))
@@ -65,8 +67,8 @@ def tile_cluster_assigner_pa_t_kernel(tc, x, cluster_emb, W, b, noise, out_0, ou
                 in_=raw[:].rearrange("p t (c i) -> p c t i", i=4),
             )
             st[("xg", k)] = g
-            if k + 5 < UNITS:
-                load_x(k + 5)
+            if k + RAW < UNITS:
+                load_x(k + RAW)
 
         def quant_x(k):
             g = st.pop(("xg", k))
@@ -77,9 +79,9 @@ def tile_cluster_assigner_pa_t_kernel(tc, x, cluster_emb, W, b, noise, out_0, ou
             )
             st[("xc", k)] = (codes, scales)
 
-        def rsqrt_clamped(out, in_, width):
+        def rsqrt_clamped(out, in_, width, eng):
             cl = small.tile([P, 4], F32, name="cl")
-            nc.gpsimd.tensor_scalar(
+            eng.tensor_scalar(
                 out=cl[:, 0:width], in0=in_, scalar1=3.0e38, scalar2=1e-24, op0=ALU.min, op1=ALU.max
             )
             nc.gpsimd.tensor_tensor(out=out, in0=cl[:, 0:width], in1=mhalf[:, 0:width], op=ALU.pow)
@@ -106,9 +108,14 @@ def tile_cluster_assigner_pa_t_kernel(tc, x, cluster_emb, W, b, noise, out_0, ou
             xe = st[("xe", k)]
             for jj in (2 * half, 2 * half + 1):
                 e = st.pop(("e", k, jj))
-                nc.scalar.activation(
-                    out=xe[:, jj, :], in_=e[:], func=ACT.Identity, bias=bcol[:, jj : jj + 1]
-                )
+                if k >= UNITS - AHEAD and jj == 3:
+                    nc.vector.tensor_scalar(
+                        out=xe[:, jj, :], in0=e[:], scalar1=bcol[:, jj : jj + 1], scalar2=None, op0=ALU.add
+                    )
+                else:
+                    nc.scalar.activation(
+                        out=xe[:, jj, :], in_=e[:], func=ACT.Identity, bias=bcol[:, jj : jj + 1]
+                    )
 
         def turn(k, i):
             xe = st[("xe", k)]
@@ -127,10 +134,10 @@ def tile_cluster_assigner_pa_t_kernel(tc, x, cluster_emb, W, b, noise, out_0, ou
                 out=junk[:], in_=xt[:].rearrange("p j d -> p (j d)"), func=ACT.Square, accum_out=ss[:, i : i + 1]
             )
 
-        def norms(k):
+        def norms(k, eng):
             ss = st.pop(("ss", k))
             rn = small.tile([P, 4], F32, name="rn")
-            rsqrt_clamped(rn[:], ss[:], 4)
+            rsqrt_clamped(rn[:], ss[:], 4, eng)
             st[("rn", k)] = rn
 
         def spread(k):
@@ -169,7 +176,7 @@ def tile_cluster_assigner_pa_t_kernel(tc, x, cluster_emb, W, b, noise, out_0, ou
             st[("c2", k)] = (c2, s2t)
 
         def s2(vb, t):
-            if t == 0:
+            if t == 0 and vb < NVB - 1:
                 m4 = psm.tile([P, TPB, C], F32, name="m4")
                 st[("m4", vb)] = m4
             m4 = st[("m4", vb)]
@@ -192,55 +199,94 @@ def tile_cluster_assigner_pa_t_kernel(tc, x, cluster_emb, W, b, noise, out_0, ou
                 st[("pa", vb)] = epi.tile([P, TPB, C], F32, name="pa")
                 st[("mask", vb)] = epi.tile([P, TPB, C], F32, name="mask")
             q = st[("q", vb)]
-            z = small.tile([P, 1], F32, name="z")
-            nc.scalar.activation(out=q[:, t, :], in_=m4[:, t, :], func=ACT.Exp, scale=5.0, accum_out=z[:])
-            st[("z", vb, t)] = z
+            h, i = divmod(t, 2)
+            if i == 0:
+                st[("z", vb, h)] = small.tile([P, 2], F32, name="z")
+            z = st[("z", vb, h)]
+            nc.scalar.activation(
+                out=q[:, t, :], in_=m4[:, t, :], func=ACT.Exp, scale=5.0, accum_out=z[:, i : i + 1]
+            )
 
-        def ep_rz(vb, t):
-            z = st.pop(("z", vb, t))
-            rz = small.tile([P, 1], F32, name="rz")
+        def ep_rz(vb, h):
+            z = st.pop(("z", vb, h))
+            rz = small.tile([P, 2], F32, name="rz")
             nc.vector.reciprocal(out=rz[:], in_=z[:])
-            st[("rz", vb, t)] = rz
+            st[("rz", vb, h)] = rz
 
         def ep_pa(vb, t):
             q = st[("q", vb)]
             pa = st[("pa", vb)]
-            rz = st.pop(("rz", vb, t))
-            nc.scalar.activation(out=pa[:, t, :], in_=q[:, t, :], func=ACT.Copy, scale=rz[:])
+            rz = st[("rz", vb, t // 2)]
+            nc.scalar.activation(
+                out=pa[:, t, :], in_=q[:, t, :], func=ACT.Copy, scale=rz[:, t % 2 : t % 2 + 1]
+            )
             if t == TPB - 1:
                 nc.sync.dma_start(out=out_0[vb * VB : (vb + 1) * VB, :].rearrange("(t p) c -> p t c", p=P), in_=pa[:])
 
-        def ep_b(vb, t, eng):
+        def ep_t(vb, h):
             pa = st[("pa", vb)]
-            tile = vb * TPB + t
-            t1 = epi4.tile([P, C], F32, name="t1")
+            two = slice(2 * h, 2 * h + 2)
+            tiles = slice(vb * TPB + 2 * h, vb * TPB + 2 * h + 2)
+            t1 = epi4.tile([P, 2, C], F32, name="t1")
             nc.vector.scalar_tensor_tensor(
-                out=t1[:], in0=pa[:, t, :], scalar=EPS, in1=u[:, tile, :], op0=ALU.add, op1=ALU.mult
+                out=t1[:], in0=pa[:, two, :], scalar=EPS, in1=u[:, tiles, :], op0=ALU.add, op1=ALU.mult
             )
-            t2 = epi4.tile([P, C], F32, name="t2")
+            t2 = epi4.tile([P, 2, C], F32, name="t2")
             nc.vector.scalar_tensor_tensor(
-                out=t2[:], in0=pa[:, t, :], scalar=-(1.0 + EPS), in1=um1[:, tile, :], op0=ALU.add, op1=ALU.mult
+                out=t2[:], in0=pa[:, two, :], scalar=-(1.0 + EPS), in1=um1[:, tiles, :], op0=ALU.add, op1=ALU.mult
             )
-            den = epi4.tile([P, C], F32, name="den")
-            eng.tensor_tensor(out=den[:], in0=t1[:], in1=t2[:], op=ALU.add)
-            st[("den", vb, t)] = (t1, den)
+            st[("t", vb, h)] = (t1, t2)
 
-        def ep_c(vb, t, eng):
-            t1, den = st.pop(("den", vb, t))
-            rden = epi4.tile([P, C], F32, name="rden")
-            nc.vector.reciprocal(out=rden[:], in_=den[:])
+        def ep_den(vb, h, eng):
+            t1, t2 = st.pop(("t", vb, h))
+            den = epi4.tile([P, 2, C], F32, name="den")
+            eng.tensor_tensor(out=den[:], in0=t1[:], in1=t2[:], op=ALU.add)
+            st[("den", vb, h)] = (t1, den)
+
+        def ep_prod(vb, h, eng):
+            t1, den = st[("den", vb, h)]
+            prod = epi4.tile([P, C], F32, name="prod")
+            eng.tensor_tensor(out=prod[:], in0=den[:, 0, :], in1=den[:, 1, :], op=ALU.mult)
+            st[("prod", vb, h)] = prod
+
+        def ep_cross(vb, h, eng):
+            t1, den = st.pop(("den", vb, h))
+            cross = epi4.tile([P, 2, C], F32, name="cross")
+            eng.tensor_tensor(out=cross[:], in0=t1[:], in1=den[:, ::-1, :], op=ALU.mult)
+            st[("cross", vb, h)] = cross
+
+        def ep_rec(vb, h):
+            prod = st.pop(("prod", vb, h))
+            rec = epi4.tile([P, C], F32, name="rec")
+            nc.vector.reciprocal(out=rec[:], in_=prod[:])
+            st[("rec", vb, h)] = rec
+
+        def ep_mask(vb, h, eng):
+            cross = st.pop(("cross", vb, h))
+            rec = st.pop(("rec", vb, h))
             mask = st[("mask", vb)]
-            eng.tensor_tensor(out=mask[:, t, :], in0=t1[:], in1=rden[:], op=ALU.mult)
-            if t == TPB - 1:
+            eng.tensor_tensor(
+                out=mask[:, 2 * h : 2 * h + 2, :],
+                in0=cross[:],
+                in1=rec[:].unsqueeze(1).to_broadcast([P, 2, C]),
+                op=ALU.mult,
+            )
+            if h == 1:
                 nc.sync.dma_start(out=out_1[vb * VB : (vb + 1) * VB, :].rearrange("(t p) c -> p t c", p=P), in_=mask[:])
 
-        w_sb = const.tile([P, 4, S], BF16, name="w_sb")
-        nc.sync.dma_start(out=w_sb[:], in_=W.rearrange("(a p) t -> p a t", p=P))
-        for k in range(5):
-            load_x(k)
         zb = const.tile([P, P], BF16, name="zb")
         nc.vector.memset(zb[:], 0.0)
+        mhalf = const.tile([P, 4], F32, name="mhalf")
+        nc.vector.memset(mhalf[:], -0.5)
+        w_sb = const.tile([P, 4, S], BF16, name="w_sb")
+        load_x(0)
+        for h in range(2):
+            nc.sync.dma_start(
+                out=w_sb[:, 2 * h : 2 * h + 2, :], in_=W[h * 2 * P : (h + 1) * 2 * P, :].rearrange("(a p) t -> p a t", p=P)
+            )
         nc.scalar.dma_start(out=zb[0:4, :], in_=b.rearrange("(j p) -> j p", p=P))
+        for k in range(1, RAW):
+            load_x(k)
         ce = const.tile([P, D], BF16, name="ce")
         nc.scalar.dma_start(out=ce[:], in_=cluster_emb)
         u = const.tile([P, V // P, C], BF16, name="u")
@@ -251,20 +297,12 @@ def tile_cluster_assigner_pa_t_kernel(tc, x, cluster_emb, W, b, noise, out_0, ou
         make_identity(nc, ident[:])
         identf = const.tile([P, P], F32, name="identf")
         make_identity(nc, identf[:])
-        mhalf = const.tile([P, 4], F32, name="mhalf")
-        nc.vector.memset(mhalf[:], -0.5)
 
-        junk0 = work.tile([P, D], BF16, name="junk")
-        ssc = small.tile([P, 4], F32, name="ss")
-        nc.scalar.activation(out=junk0[:], in_=ce[:], func=ACT.Square, accum_out=ssc[:, 0:1])
-        rc = const.tile([P, 1], F32, name="rc")
-        rsqrt_clamped(rc[:, 0:1], ssc[:, 0:1], 1)
-
-        regroup_x(0)
-        quant_x(0)
-
-        gw = const.tile([P, 4, P, 4], BF16, name="gw", align_bytes=64)
+        wc = const.tile([P, D], U32, name="wc", align_bytes=64)
+        ws = const.tile([P, D], U8, name="ws", align_bytes=64)
+        gws = []
         for h in range(2):
+            gw = const.tile([P, 2, P, 4], BF16, name="gw%d" % h, align_bytes=64)
             wt = pse.tile([P, 2, 4, P], BF16, name="e")
             for a2 in range(2):
                 for j in range(4):
@@ -273,45 +311,78 @@ def tile_cluster_assigner_pa_t_kernel(tc, x, cluster_emb, W, b, noise, out_0, ou
                         w_sb[:, 2 * h + a2, :].rearrange("p (q j) -> p j q", j=4)[:, j, :],
                         ident[:],
                     )
-            nc.scalar.copy(
-                out=gw[:, 2 * h : 2 * h + 2, :, :], in_=wt[:].rearrange("p a j d -> p a d j")
+            nc.scalar.copy(out=gw[:], in_=wt[:].rearrange("p a j d -> p a d j"))
+            gws.append(gw)
+
+        def quant_w(h):
+            cols = slice(2 * h * P, 2 * (h + 1) * P)
+            nc.vector.quantize_mx(
+                out=wc[:, cols].bitcast(FP8X4), scales=ws[:, cols], in_=gws[h][:].rearrange("p a d j -> p (a d j)")
             )
-        wc = const.tile([P, D], U32, name="wc", align_bytes=64)
-        ws = const.tile([P, D], U8, name="ws", align_bytes=64)
-        nc.vector.quantize_mx(
-            out=wc[:].bitcast(FP8X4), scales=ws[:], in_=gw[:].rearrange("p a d j -> p (a d j)")
-        )
+
         bt = pse.tile([P, P], BF16, name="e")
         nc.tensor.transpose(bt[:], zb[:], ident[:])
         bcol = const.tile([P, 4], F32, name="bcol")
-        nc.vector.tensor_copy(out=bcol[:], in_=bt[:, 0:4])
+        nc.scalar.copy(out=bcol[:], in_=bt[:, 0:4])
 
         cn = const.tile([P, D], BF16, name="cn")
         gc = const.tile([P, C, 4], BF16, name="gc", align_bytes=64)
         cc = const.tile([P, C], U32, name="cc", align_bytes=64)
         cs = const.tile([P, C], U8, name="cs", align_bytes=64)
+        ssc = const.tile([P, 1], F32, name="ssc")
+        rc = const.tile([P, 1], F32, name="rc")
 
+        xq = {"r": 0, "q": 0, "n": 0}
+
+        def x_step():
+            xq["n"] += 1
+            if xq["r"] < UNITS:
+                regroup_x(xq["r"])
+                xq["r"] += 1
+            if xq["q"] < UNITS and xq["r"] >= 2:
+                quant_x(xq["q"])
+                xq["q"] += 1
+
+        def on(k):
+            return 0 <= k < UNITS
+
+        x_step()
+        x_step()
+        quant_w(0)
         s1(0, 0)
+        x_step()
+        quant_w(1)
         s1(0, 1)
-        regroup_x(1)
-        regroup_x(2)
-        quant_x(1)
-        regroup_x(3)
-        quant_x(2)
 
-        def blk(e):
-            return divmod(e, TPB)
+        plan = {}
 
-        for j in range(UNITS + 8):
-            def on(k):
-                return 0 <= k < UNITS
-            def ep(k):
-                return 0 <= k < UNITS - TPB
+        def at(j, step, vb, i):
+            plan.setdefault((j, step), []).append((vb, i))
+
+        for vb in range(NVB - 1):
+            for t in range(TPB):
+                first = vb * NB + 7 + t
+                if vb == NVB - 2:
+                    first = UNITS - 1 + t // 2
+                at(first, "s2", vb, t)
+                at(first + 1, "exp", vb, t)
+            for h in range(2):
+                first = vb * NB + 7 + 2 * h + 2
+                lag = (0, 1, 2, 3, 4, 5) if first + 4 < UNITS + 3 else (0, 1, 2, 2, 3, 3)
+                if vb == NVB - 2:
+                    first = UNITS + h
+                    lag = (0, 1, 1, 2, 3, 3) if h == 0 else (0, 1, 2, 2, 2, 2)
+                for step, dj in zip(("rz", "pa", "t", "cross", "rec", "mask"), lag):
+                    at(first + dj, step, vb, h)
+
+        for j in range(UNITS + 3):
             if on(j - 3):
                 final(j - 3)
-            if j < UNITS:
+            for e in plan.get((j, "rec"), ()):
+                ep_rec(*e)
+            if on(j):
                 evac(j, 0)
-            if j + 1 < UNITS:
+            if on(j + 1):
                 s1(j + 1, 0)
             if on(j - 1):
                 square_sum(j - 1, 0)
@@ -320,63 +391,87 @@ def tile_cluster_assigner_pa_t_kernel(tc, x, cluster_emb, W, b, noise, out_0, ou
                 turn(j - 1, 3)
             if on(j - 2):
                 spread(j - 2)
-            if j < UNITS:
+            for e in plan.get((j, "exp"), ()):
+                ep_exp(*e)
+            if on(j):
                 evac(j, 1)
-            if j + 1 < UNITS:
+            if on(j + 1):
                 s1(j + 1, 1)
-            if ep(j - 7):
-                s2(*blk(j - 7))
+            for e in plan.get((j, "s2"), ()):
+                s2(*e)
             if on(j - 1):
                 square_sum(j - 1, 2)
                 square_sum(j - 1, 3)
-            if j < UNITS:
+            if on(j):
                 turn(j, 0)
                 turn(j, 1)
-            if ep(j - 8):
-                ep_exp(*blk(j - 8))
-            if ep(j - 9):
-                ep_rz(*blk(j - 9))
-            if ep(j - 10):
-                ep_pa(*blk(j - 10))
+            for e in plan.get((j, "pa"), ()):
+                for i in range(2):
+                    ep_pa(e[0], 2 * e[1] + i)
             if j % NB == 0 and j < UNITS:
                 tiles = slice(j, j + NB)
                 nc.scalar.activation(out=um1[:, tiles, :], in_=u[:, tiles, :], func=ACT.Copy, bias=-1.0)
-            if j == 1:
-                nc.scalar.copy(out=gc[:], in_=st.pop("ct")[:, 0, :, :].rearrange("p t c -> p c t"))
             if j == 0:
-                nc.vector.tensor_scalar(out=cn[:], in0=ce[:], scalar1=rc[:, 0:1], scalar2=None, op0=ALU.mult)
-                ct = psm.tile([P, 2, 4, P], BF16, name="m4")
+                junk = sqp.tile([P, D], BF16, name="sq")
+                nc.scalar.activation(out=junk[:], in_=ce[:], func=ACT.Square, accum_out=ssc[:])
+                rsqrt_clamped(rc[:], ssc[:], 1, nc.gpsimd)
+            if j == 1:
+                nc.vector.tensor_scalar(out=cn[:], in0=ce[:], scalar1=rc[:], scalar2=None, op0=ALU.mult)
+                ct = psm.tile([P, 4, P], BF16, name="m4")
                 for t in range(4):
-                    nc.tensor.transpose(ct[:, 0, t, :], cn[:, t * P : (t + 1) * P], ident[:])
+                    nc.tensor.transpose(ct[:, t, :], cn[:, t * P : (t + 1) * P], ident[:])
                 st["ct"] = ct
-            if j + 4 < UNITS:
-                regroup_x(j + 4)
             if j == 2:
+                nc.scalar.copy(out=gc[:], in_=st.pop("ct")[:].rearrange("p t c -> p c t"))
+            while xq["n"] < min(UNITS + 1, AHEAD + j):
+                x_step()
+            if j == 4:
                 nc.vector.quantize_mx(
                     out=cc[:].bitcast(FP8X4), scales=cs[:], in_=gc[:].rearrange("p c t -> p (c t)")
                 )
             if on(j - 3):
                 quant_xn(j - 3)
-            if j + 3 < UNITS:
-                quant_x(j + 3)
-            if ep(j - 11):
-                ep_b(*blk(j - 11), nc.gpsimd)
+            for e in plan.get((j, "rz"), ()):
+                ep_rz(*e)
+            for e in plan.get((j, "t"), ()):
+                ep_t(*e)
+                ep_den(*e, nc.vector if e in plan.get((j, "cross"), ()) else nc.gpsimd)
+            for e in plan.get((j, "cross"), ()):
+                ep_prod(*e, nc.vector)
             if on(j - 1):
-                norms(j - 1)
-            if ep(j - 12):
-                ep_c(*blk(j - 12), nc.gpsimd)
-            if j == UNITS + 3:
-                for t in range(TPB):
-                    s2(NVB - 1, t)
+                norms(j - 1, nc.gpsimd if j < 12 or j > UNITS - 6 else nc.vector)
+            for e in plan.get((j, "cross"), ()):
+                ep_cross(*e, nc.gpsimd)
+            for e in plan.get((j, "mask"), ()):
+                ep_mask(*e, nc.gpsimd)
 
         last = NVB - 1
+        banks = (psm.tile([P, TPB, C], F32, name="m4"), pse.tile([P, TPB, C], F32, name="e"))
         for t in range(TPB):
+            st[("m4", last)] = banks[t // 2]
+            s2(last, t)
+        for t in range(TPB):
+            st[("m4", last)] = banks[t // 2]
             ep_exp(last, t)
-        for t in range(TPB):
-            ep_rz(last, t)
-        for t in range(TPB):
-            ep_pa(last, t)
-        for t in range(TPB):
-            ep_b(last, t, nc.vector)
-        for t in range(TPB):
-            ep_c(last, t, nc.vector)
+        ep_t(last - 1, 1)
+        ep_rec(last - 1, 0)
+        ep_den(last - 1, 1, nc.vector)
+        ep_mask(last - 1, 0, nc.gpsimd)
+        ep_prod(last - 1, 1, nc.vector)
+        ep_cross(last - 1, 1, nc.gpsimd)
+        ep_rec(last - 1, 1)
+        ep_mask(last - 1, 1, nc.gpsimd)
+        for h in range(2):
+            ep_rz(last, h)
+            ep_pa(last, 2 * h)
+            ep_pa(last, 2 * h + 1)
+        for h in range(2):
+            ep_t(last, h)
+            ep_den(last, h, nc.vector)
+        for h in range(2):
+            ep_prod(last, h, nc.vector)
+            ep_cross(last, h, nc.gpsimd)
+        for h in range(2):
+            ep_rec(last, h)
+        for h in range(2):
+            ep_mask(last, h, nc.vector)

@@ -90,6 +90,8 @@ def tile_cluster_assigner_pa_t_kernel(tc, x, cluster_emb, W, b, noise, out_0, ou
             codes, scales = st[("xc", k)]
             for jj in (2 * half, 2 * half + 1):
                 e = pse.tile([P, VB], F32, name="e")
+                for i in range(1):
+                    nc.tensor.matmul(out=e[:, 0:128], lhsT=identf[:], rhs=identf[:, 0:128], start=True, stop=True)
                 nc.tensor.matmul_mx(
                     out=e[:],
                     lhsT=wc[:, jj * P : (jj + 1) * P].bitcast(FP8X4),
@@ -285,12 +287,13 @@ def tile_cluster_assigner_pa_t_kernel(tc, x, cluster_emb, W, b, noise, out_0, ou
                 out=w_sb[:, 2 * h : 2 * h + 2, :], in_=W[h * 2 * P : (h + 1) * 2 * P, :].rearrange("(a p) t -> p a t", p=P)
             )
         nc.scalar.dma_start(out=zb[0:4, :], in_=b.rearrange("(j p) -> j p", p=P))
-        for k in range(1, RAW):
+        for k in range(1, 3):
             load_x(k)
         ce = const.tile([P, D], BF16, name="ce")
-        nc.scalar.dma_start(out=ce[:], in_=cluster_emb)
+        nc.sync.dma_start(out=ce[:], in_=cluster_emb)
+        for k in range(3, RAW):
+            load_x(k)
         u = const.tile([P, V // P, C], BF16, name="u")
-        nc.gpsimd.dma_start(out=u[:], in_=noise.rearrange("(t p) c -> p t c", p=P))
         um1 = const.tile([P, V // P, C], F32, name="um1")
 
         ident = const.tile([P, P], BF16, name="ident")
@@ -408,8 +411,10 @@ def tile_cluster_assigner_pa_t_kernel(tc, x, cluster_emb, W, b, noise, out_0, ou
             for e in plan.get((j, "pa"), ()):
                 for i in range(2):
                     ep_pa(e[0], 2 * e[1] + i)
-            if j % NB == 0 and j < UNITS:
-                tiles = slice(j, j + NB)
+            if j == 0:
+                nc.sync.dma_start(out=u[:], in_=noise.rearrange("(t p) c -> p t c", p=P))
+            if j % NB == 2 and j > NB:
+                tiles = slice(j - NB - 2, j - 2)
                 nc.scalar.activation(out=um1[:, tiles, :], in_=u[:, tiles, :], func=ACT.Copy, bias=-1.0)
             if j == 0:
                 junk = sqp.tile([P, D], BF16, name="sq")

from contextlib import ExitStack

import concourse.mybir as mybir
from concourse.masks import make_identity

F32 = mybir.dt.float32
BF16 = mybir.dt.bfloat16
U32 = mybir.dt.uint32
U8 = mybir.dt.uint8
FP8X4 = mybir.dt.float8_e4m3fn_x4
ALU = mybir.AluOpType
ACT = mybir.ActivationFunctionType

P = 128
NB = 4
S = 512
V = 4096
C = 128
D = 512
VB = 512
NVB = V // VB
TPB = VB // P
UNITS = NB * NVB
EPS = 1e-10
RAW = 5
AHEAD = 7

FLOPS = 2 * NB * V * S * D + 2 * NB * V * D * C


def tile_cluster_assigner_pa_t_kernel(tc, x, cluster_emb, W, b, noise, out_0, out_1):
    nc = tc.nc
    with ExitStack() as ctx:
        const = ctx.enter_context(tc.tile_pool(name="const", bufs=1))
        rawp = ctx.enter_context(tc.tile_pool(name="rawp", bufs=RAW))
        xgp = ctx.enter_context(tc.tile_pool(name="xgp", bufs=3))
        xcp = ctx.enter_context(tc.tile_pool(name="xcp", bufs=12))
        xep = ctx.enter_context(tc.tile_pool(name="xep", bufs=5))
        sqp = ctx.enter_context(tc.tile_pool(name="sqp", bufs=2))
        work = ctx.enter_context(tc.tile_pool(name="work", bufs=2))
        c2p = ctx.enter_context(tc.tile_pool(name="c2p", bufs=12))
        small = ctx.enter_context(tc.tile_pool(name="small", bufs=6))
        epi = ctx.enter_context(tc.tile_pool(name="epi", bufs=2))
        epi4 = ctx.enter_context(tc.tile_pool(name="epi4", bufs=4))
        pse = ctx.enter_context(tc.psum_pool(name="pse", bufs=4))
        psa = ctx.enter_context(tc.psum_pool(name="psa", bufs=2))
        psr = ctx.enter_context(tc.psum_pool(name="psr", bufs=1))
        psm = ctx.enter_context(tc.psum_pool(name="psm", bufs=1))
        ctx.enter_context(tc.manual_schedule())

        st = {}

        def load_x(k):
            vb, n = divmod(k, NB)
            raw = rawp.tile([P, 4, VB], BF16, name="raw")
            nc.sync.dma_start(
                out=raw[:],
                in_=x[n, :, vb * VB : (vb + 1) * VB].rearrange("(p j) w -> p j w", j=4),
            )
            st[("raw", k)] = raw

        def regroup_x(k):
            raw = st.pop(("raw", k))
            g = xgp.tile([P, VB, 4], BF16, name="xg", align_bytes=64)
            nc.vector.tensor_copy(
                out=g[:].rearrange("p (c i) t -> p c t i", i=4),
                in_=raw[:].rearrange("p t (c i) -> p c t i", i=4),
            )
            st[("xg", k)] = g
            if k + RAW < UNITS:
                load_x(k + RAW)

        def quant_x(k):
            g = st.pop(("xg", k))
            codes = xcp.tile([P, VB], U32, name="xcodes", align_bytes=64)
            scales = xcp.tile([P, VB], U8, name="xscales", align_bytes=64)
            nc.vector.quantize_mx(
                out=codes[:].bitcast(FP8X4), scales=scales[:], in_=g[:].rearrange("p w t -> p (w t)")
            )
            st[("xc", k)] = (codes, scales)

        def rsqrt_clamped(out, in_, width, eng):
            cl = small.tile([P, 4], F32, name="cl")
            eng.tensor_scalar(
                out=cl[:, 0:width], in0=in_, scalar1=3.0e38, scalar2=1e-24, op0=ALU.min, op1=ALU.max
            )
            nc.gpsimd.tensor_tensor(out=out, in0=cl[:, 0:width], in1=mhalf[:, 0:width], op=ALU.pow)

        def s1(k, half):
            codes, scales = st[("xc", k)]
            for jj in (2 * half, 2 * half + 1):
                e = pse.tile([P, VB], F32, name="e")
                for i in range(1):
                    nc.tensor.matmul(out=e[:, 0:128], lhsT=identf[:], rhs=identf[:, 0:128], start=True, stop=True)
                nc.tensor.matmul_mx(
                    out=e[:],
                    lhsT=wc[:, jj * P : (jj + 1) * P].bitcast(FP8X4),
                    lhsT_scale=ws[:, jj * P : (jj + 1) * P],
                    rhs=codes[:].bitcast(FP8X4),
                    rhs_scale=scales[:],
                    start=True,
                    stop=True,
                )
                st[("e", k, jj)] = e

        def evac(k, half):
            if half == 0:
                xe = xep.tile([P, 4, VB], F32, name="xe")
                st[("xe", k)] = xe
            xe = st[("xe", k)]
            for jj in (2 * half, 2 * half + 1):
                e = st.pop(("e", k, jj))
                if k >= UNITS - AHEAD and jj == 3:
                    nc.vector.tensor_scalar(
                        out=xe[:, jj, :], in0=e[:], scalar1=bcol[:, jj : jj + 1], scalar2=None, op0=ALU.add
                    )
                else:
                    nc.scalar.activation(
                        out=xe[:, jj, :], in_=e[:], func=ACT.Identity, bias=bcol[:, jj : jj + 1]
                    )

        def turn(k, i):
            xe = st[("xe", k)]
            xt = psa.tile([P, 4, P], F32, name="xt")
            for jj in range(4):
                nc.tensor.transpose(xt[:, jj, :], xe[:, jj, i * P : (i + 1) * P], identf[:])
            st[("xt", k, i)] = xt

        def square_sum(k, i):
            if i == 0:
                st[("ss", k)] = small.tile([P, 4], F32, name="ss")
            ss = st[("ss", k)]
            xt = st.pop(("xt", k, i))
            junk = sqp.tile([P, D], BF16, name="sq")
            nc.scalar.activation(
                out=junk[:], in_=xt[:].rearrange("p j d -> p (j d)"), func=ACT.Square, accum_out=ss[:, i : i + 1]
            )

        def norms(k, eng):
            ss = st.pop(("ss", k))
            rn = small.tile([P, 4], F32, name="rn")
            rsqrt_clamped(rn[:], ss[:], 4, eng)
            st[("rn", k)] = rn

        def spread(k):
            rn = st.pop(("rn", k))
            rnb = psr.tile([P, VB], F32, name="bank")
            for i in range(TPB):
                nc.tensor.matmul(
                    out=rnb[:, i * P : (i + 1) * P],
                    lhsT=rn[:, i : i + 1].to_broadcast([P, P]),
                    rhs=identf[:],
                    is_transpose=True,
                    start=True,
                    stop=True,
                )
            st[("rnb", k)] = rnb

        def final(k):
            xe = st.pop(("xe", k))
            rnb = st.pop(("rnb", k))
            g2 = work.tile([P, VB, 4], BF16, name="g2", align_bytes=64)
            nc.vector.tensor_tensor(
                out=g2[:].rearrange("p (c i) j -> p c j i", i=4),
                in0=xe[:].rearrange("p j (c i) -> p c j i", i=4),
                in1=rnb[:].rearrange("p (c i) -> p c i", i=4).unsqueeze(2).to_broadcast([P, VB // 4, 4, 4]),
                op=ALU.mult,
            )
            st[("g2", k)] = g2

        def quant_xn(k):
            g2 = st.pop(("g2", k))
            c2 = c2p.tile([P, VB], U32, name="c2", align_bytes=64)
            s2t = c2p.tile([P, VB], U8, name="s2t", align_bytes=64)
            nc.vector.quantize_mx(
                out=c2[:].bitcast(FP8X4), scales=s2t[:], in_=g2[:].rearrange("p v j -> p (v j)")
            )
            st[("c2", k)] = (c2, s2t)

        def s2(vb, t):
            if t == 0 and vb < NVB - 1:
                m4 = psm.tile([P, TPB, C], F32, name="m4")
                st[("m4", vb)] = m4
            m4 = st[("m4", vb)]
            for n in range(NB):
                c2, s2t = st[("c2", vb * NB + n)]
                nc.tensor.matmul_mx(
                    out=m4[:, t, :],
                    lhsT=c2[:, t * P : (t + 1) * P].bitcast(FP8X4),
                    lhsT_scale=s2t[:, t * P : (t + 1) * P],
                    rhs=cc[:].bitcast(FP8X4),
                    rhs_scale=cs[:],
                    start=(n == 0),
                    stop=(n == NB - 1),
                )

        def ep_exp(vb, t):
            m4 = st[("m4", vb)]
            if t == 0:
                st[("q", vb)] = epi.tile([P, TPB, C], F32, name="q")
                st[("pa", vb)] = epi.tile([P, TPB, C], F32, name="pa")
                st[("mask", vb)] = epi.tile([P, TPB, C], F32, name="mask")
            q = st[("q", vb)]
            h, i = divmod(t, 2)
            if i == 0:
                st[("z", vb, h)] = small.tile([P, 2], F32, name="z")
            z = st[("z", vb, h)]
            nc.scalar.activation(
                out=q[:, t, :], in_=m4[:, t, :], func=ACT.Exp, scale=5.0, accum_out=z[:, i : i + 1]
            )

        def ep_rz(vb, h):
            z = st.pop(("z", vb, h))
            rz = small.tile([P, 2], F32, name="rz")
            nc.vector.reciprocal(out=rz[:], in_=z[:])
            st[("rz", vb, h)] = rz

        def ep_pa(vb, t):
            q = st[("q", vb)]
            pa = st[("pa", vb)]
            rz = st[("rz", vb, t // 2)]
            nc.scalar.activation(
                out=pa[:, t, :], in_=q[:, t, :], func=ACT.Copy, scale=rz[:, t % 2 : t % 2 + 1]
            )
            if t == TPB - 1:
                nc.sync.dma_start(out=out_0[vb * VB : (vb + 1) * VB, :].rearrange("(t p) c -> p t c", p=P), in_=pa[:])

        def ep_t(vb, h):
            pa = st[("pa", vb)]
            two = slice(2 * h, 2 * h + 2)
            tiles = slice(vb * TPB + 2 * h, vb * TPB + 2 * h + 2)
            t1 = epi4.tile([P, 2, C], F32, name="t1")
            nc.vector.scalar_tensor_tensor(
                out=t1[:], in0=pa[:, two, :], scalar=EPS, in1=u[:, tiles, :], op0=ALU.add, op1=ALU.mult
            )
            t2 = epi4.tile([P, 2, C], F32, name="t2")
            nc.vector.scalar_tensor_tensor(
                out=t2[:], in0=pa[:, two, :], scalar=-(1.0 + EPS), in1=um1[:, tiles, :], op0=ALU.add, op1=ALU.mult
            )
            st[("t", vb, h)] = (t1, t2)

        def ep_den(vb, h, eng):
            t1, t2 = st.pop(("t", vb, h))
            den = epi4.tile([P, 2, C], F32, name="den")
            eng.tensor_tensor(out=den[:], in0=t1[:], in1=t2[:], op=ALU.add)
            st[("den", vb, h)] = (t1, den)

        def ep_prod(vb, h, eng):
            t1, den = st[("den", vb, h)]
            prod = epi4.tile([P, C], F32, name="prod")
            eng.tensor_tensor(out=prod[:], in0=den[:, 0, :], in1=den[:, 1, :], op=ALU.mult)
            st[("prod", vb, h)] = prod

        def ep_cross(vb, h, eng):
            t1, den = st.pop(("den", vb, h))
            cross = epi4.tile([P, 2, C], F32, name="cross")
            eng.tensor_tensor(out=cross[:], in0=t1[:], in1=den[:, ::-1, :], op=ALU.mult)
            st[("cross", vb, h)] = cross

        def ep_rec(vb, h):
            prod = st.pop(("prod", vb, h))
            rec = epi4.tile([P, C], F32, name="rec")
            nc.vector.reciprocal(out=rec[:], in_=prod[:])
            st[("rec", vb, h)] = rec

        def ep_mask(vb, h, eng):
            cross = st.pop(("cross", vb, h))
            rec = st.pop(("rec", vb, h))
            mask = st[("mask", vb)]
            eng.tensor_tensor(
                out=mask[:, 2 * h : 2 * h + 2, :],
                in0=cross[:],
                in1=rec[:].unsqueeze(1).to_broadcast([P, 2, C]),
                op=ALU.mult,
            )
            if h == 1:
                nc.sync.dma_start(out=out_1[vb * VB : (vb + 1) * VB, :].rearrange("(t p) c -> p t c", p=P), in_=mask[:])

        zb = const.tile([P, P], BF16, name="zb")
        nc.vector.memset(zb[:], 0.0)
        mhalf = const.tile([P, 4], F32, name="mhalf")
        nc.vector.memset(mhalf[:], -0.5)
        w_sb = const.tile([P, 4, S], BF16, name="w_sb")
        load_x(0)
        for h in range(2):
            nc.sync.dma_start(
                out=w_sb[:, 2 * h : 2 * h + 2, :], in_=W[h * 2 * P : (h + 1) * 2 * P, :].rearrange("(a p) t -> p a t", p=P)
            )
        nc.scalar.dma_start(out=zb[0:4, :], in_=b.rearrange("(j p) -> j p", p=P))
        for k in range(1, 3):
            load_x(k)
        ce = const.tile([P, D], BF16, name="ce")
        nc.sync.dma_start(out=ce[:], in_=cluster_emb)
        for k in range(3, RAW):
            load_x(k)
        u = const.tile([P, V // P, C], BF16, name="u")
        um1 = const.tile([P, V // P, C], F32, name="um1")

        ident = const.tile([P, P], BF16, name="ident")
        make_identity(nc, ident[:])
        identf = const.tile([P, P], F32, name="identf")
        make_identity(nc, identf[:])

        wc = const.tile([P, D], U32, name="wc", align_bytes=64)
        ws = const.tile([P, D], U8, name="ws", align_bytes=64)
        gws = []
        for h in range(2):
            gw = const.tile([P, 2, P, 4], BF16, name="gw%d" % h, align_bytes=64)
            wt = pse.tile([P, 2, 4, P], BF16, name="e")
            for a2 in range(2):
                for j in range(4):
                    nc.tensor.transpose(
                        wt[:, a2, j, :],
                        w_sb[:, 2 * h + a2, :].rearrange("p (q j) -> p j q", j=4)[:, j, :],
                        ident[:],
                    )
            nc.scalar.copy(out=gw[:], in_=wt[:].rearrange("p a j d -> p a d j"))
            gws.append(gw)

        def quant_w(h):
            cols = slice(2 * h * P, 2 * (h + 1) * P)
            nc.vector.quantize_mx(
                out=wc[:, cols].bitcast(FP8X4), scales=ws[:, cols], in_=gws[h][:].rearrange("p a d j -> p (a d j)")
            )

        bt = pse.tile([P, P], BF16, name="e")
        nc.tensor.transpose(bt[:], zb[:], ident[:])
        bcol = const.tile([P, 4], F32, name="bcol")
        nc.scalar.copy(out=bcol[:], in_=bt[:, 0:4])

        cn = const.tile([P, D], BF16, name="cn")
        gc = const.tile([P, C, 4], BF16, name="gc", align_bytes=64)
        cc = const.tile([P, C], U32, name="cc", align_bytes=64)
        cs = const.tile([P, C], U8, name="cs", align_bytes=64)
        ssc = const.tile([P, 1], F32, name="ssc")
        rc = const.tile([P, 1], F32, name="rc")

        xq = {"r": 0, "q": 0, "n": 0}

        def x_step():
            xq["n"] += 1
            if xq["r"] < UNITS:
                regroup_x(xq["r"])
                xq["r"] += 1
            if xq["q"] < UNITS and xq["r"] >= 2:
                quant_x(xq["q"])
                xq["q"] += 1

        def on(k):
            return 0 <= k < UNITS

        x_step()
        x_step()
        quant_w(0)
        s1(0, 0)
        x_step()
        quant_w(1)
        s1(0, 1)

        plan = {}

        def at(j, step, vb, i):
            plan.setdefault((j, step), []).append((vb, i))

        for vb in range(NVB - 1):
            for t in range(TPB):
                first = vb * NB + 7 + t
                if vb == NVB - 2:
                    first = UNITS - 1 + t // 2
                at(first, "s2", vb, t)
                at(first + 1, "exp", vb, t)
            for h in range(2):
                first = vb * NB + 7 + 2 * h + 2
                lag = (0, 1, 2, 3, 4, 5) if first + 4 < UNITS + 3 else (0, 1, 2, 2, 3, 3)
                if vb == NVB - 2:
                    first = UNITS + h
                    lag = (0, 1, 1, 2, 3, 3) if h == 0 else (0, 1, 2, 2, 2, 2)
                for step, dj in zip(("rz", "pa", "t", "cross", "rec", "mask"), lag):
                    at(first + dj, step, vb, h)

        for j in range(UNITS + 3):
            if on(j - 3):
                final(j - 3)
            for e in plan.get((j, "rec"), ()):
                ep_rec(*e)
            if on(j):
                evac(j, 0)
            if on(j + 1):
                s1(j + 1, 0)
            if on(j - 1):
                square_sum(j - 1, 0)
                square_sum(j - 1, 1)
                turn(j - 1, 2)
                turn(j - 1, 3)
            if on(j - 2):
                spread(j - 2)
            for e in plan.get((j, "exp"), ()):
                ep_exp(*e)
            if on(j):
                evac(j, 1)
            if on(j + 1):
                s1(j + 1, 1)
            for e in plan.get((j, "s2"), ()):
                s2(*e)
            if on(j - 1):
                square_sum(j - 1, 2)
                square_sum(j - 1, 3)
            if on(j):
                turn(j, 0)
                turn(j, 1)
            for e in plan.get((j, "pa"), ()):
                for i in range(2):
                    ep_pa(e[0], 2 * e[1] + i)
            if j == 0:
                nc.sync.dma_start(out=u[:], in_=noise.rearrange("(t p) c -> p t c", p=P))
            if j % NB == 2 and j > NB:
                tiles = slice(j - NB - 2, j - 2)
                nc.scalar.activation(out=um1[:, tiles, :], in_=u[:, tiles, :], func=ACT.Copy, bias=-1.0)
            if j == 0:
                junk = sqp.tile([P, D], BF16, name="sq")
                nc.scalar.activation(out=junk[:], in_=ce[:], func=ACT.Square, accum_out=ssc[:])
                rsqrt_clamped(rc[:], ssc[:], 1, nc.gpsimd)
            if j == 1:
                nc.vector.tensor_scalar(out=cn[:], in0=ce[:], scalar1=rc[:], scalar2=None, op0=ALU.mult)
                ct = psm.tile([P, 4, P], BF16, name="m4")
                for t in range(4):
                    nc.tensor.transpose(ct[:, t, :], cn[:, t * P : (t + 1) * P], ident[:])
                st["ct"] = ct
            if j == 2:
                nc.scalar.copy(out=gc[:], in_=st.pop("ct")[:].rearrange("p t c -> p c t"))
            while xq["n"] < min(UNITS + 1, AHEAD + j):
                x_step()
            if j == 4:
                nc.vector.quantize_mx(
                    out=cc[:].bitcast(FP8X4), scales=cs[:], in_=gc[:].rearrange("p c t -> p (c t)")
                )
            if on(j - 3):
                quant_xn(j - 3)
            for e in plan.get((j, "rz"), ()):
                ep_rz(*e)
            for e in plan.get((j, "t"), ()):
                ep_t(*e)
                ep_den(*e, nc.vector if e in plan.get((j, "cross"), ()) else nc.gpsimd)
            for e in plan.get((j, "cross"), ()):
                ep_prod(*e, nc.vector)
            if on(j - 1):
                norms(j - 1, nc.gpsimd if j < 12 or j > UNITS - 6 else nc.vector)
            for e in plan.get((j, "cross"), ()):
                ep_cross(*e, nc.gpsimd)
            for e in plan.get((j, "mask"), ()):
                ep_mask(*e, nc.gpsimd)

        last = NVB - 1
        banks = (psm.tile([P, TPB, C], F32, name="m4"), pse.tile([P, TPB, C], F32, name="e"))
        for t in range(TPB):
            st[("m4", last)] = banks[t // 2]
            s2(last, t)
        for t in range(TPB):
            st[("m4", last)] = banks[t // 2]
            ep_exp(last, t)
        ep_t(last - 1, 1)
        ep_rec(last - 1, 0)
        ep_den(last - 1, 1, nc.vector)
        ep_mask(last - 1, 0, nc.gpsimd)
        ep_prod(last - 1, 1, nc.vector)
        ep_cross(last - 1, 1, nc.gpsimd)
        ep_rec(last - 1, 1)
        ep_mask(last - 1, 1, nc.gpsimd)
        for h in range(2):
            ep_rz(last, h)
            ep_pa(last, 2 * h)
            ep_pa(last, 2 * h + 1)
        for h in range(2):
            ep_t(last, h)
            ep_den(last, h, nc.vector)
        for h in range(2):
            ep_prod(last, h, nc.vector)
            ep_cross(last, h, nc.gpsimd)
        for h in range(2):
            ep_rec(last, h)
        for h in range(2):
            ep_mask(last, h, nc.vector)
